import numpy as np
import ml_dtypes


def mxq(x, axis, fmt="e4m3"):
    dtype, down = {"e4m3": (ml_dtypes.float8_e4m3fn, 7), "e5m2": (ml_dtypes.float8_e5m2, 14)}[fmt]
    v = np.moveaxis(np.asarray(x, np.float32).astype(ml_dtypes.bfloat16).astype(np.float64), axis, -1)
    blocks = v.reshape(v.shape[:-1] + (-1, 32))
    amax = np.abs(blocks).max(-1, keepdims=True)
    byte = np.maximum(np.where(amax > 0, np.frexp(amax)[1] - 1 + 127, 0) - down, 1)
    scale = np.exp2(byte - 127.0)
    codes = (blocks / scale).astype(np.float32).astype(dtype).astype(np.float64)
    return np.moveaxis((codes * scale).reshape(v.shape), -1, axis)


WIDE = False


def mx_kscale(k):
    if not WIDE:
        return np.ones(k)
    levels = np.array([10, -10, 5, -5, 0])
    a = np.random.permutation(np.resize(levels, k // 512 * 4)).reshape(k // 512, 4)
    idx = np.arange(k)
    return np.exp2(a[idx // 512, idx % 128 // 32])


BF16 = ml_dtypes.bfloat16


def bf(x):
    return np.asarray(x, np.float32).astype(BF16)


def f64(x):
    return np.asarray(x).astype(np.float64)


B, N, D, F, M1, M2 = 4, 128, 512, 2048, 3, 5
D2 = D + D


def silu(v):
    return v / (1.0 + np.exp(-v))


def setup_inputs():
    s, t = mx_kscale(D), mx_kscale(D2)
    return {"h": bf(np.random.standard_normal((B, N, D)) * t[:D]),
            "x1": bf(np.random.standard_normal((B, N, D, M1)) * s[:, None]),
            "pre1": bf(np.random.standard_normal((D, D)) / np.sqrt(D) / s[:, None] * t[D:]),
            "w1_0": bf(np.random.standard_normal((D2, F)) / np.sqrt(D2) / t[:, None]),
            "b1_0": bf(np.random.standard_normal(F) * 0.2)}


def reference(h, x1, pre1, w1_0, b1_0):
    xt = f64(x1).swapaxes(-1, -2).reshape(B * N * M1, D)
    pm = (mxq(xt, 1, "e4m3") @ mxq(f64(pre1), 0, "e4m3")).reshape(B, N, M1, D)
    inv = np.sqrt(np.sum(pm * pm, axis=-2))
    mlp_in = np.concatenate([f64(h), inv], axis=-1)
    return silu((mxq(mlp_in, 2, "e4m3") @ mxq(f64(w1_0), 0, "e4m3")) + f64(b1_0))

@@ -1,0 +1,273 @@
+from contextlib import ExitStack
+
+import concourse.masks as masks
+import concourse.mybir as mybir
+
+F32 = mybir.dt.float32
+BF16 = mybir.dt.bfloat16
+U32 = mybir.dt.uint32
+U8 = mybir.dt.uint8
+FP8X4 = mybir.dt.float8_e4m3fn_x4
+ACT = mybir.ActivationFunctionType
+ALU = mybir.AluOpType
+
+P = 128
+NT = 4
+D = 512
+F = 2048
+M1 = 3
+FC = 512
+NF = F // FC
+NU = NT * M1
+FLOPS = 2 * (NT * P * M1) * D * D + 2 * (NT * P) * (2 * D) * F
+
+XE = ["V","S","V","S","S","S","V","S","V","S","S","S"]
+HE = ["S","S"]
+WE = [["V","V"],["V","V"],["V","V"],["V","S"]]
+PRE_ENG = "V"
+MANUAL = True
+ORDER = [["D","x",0],["D","pre"],["D","x",1],["D","w",0,0],["D","x",3],["D","w",0,1],["D","x",2],["D","h"],["D","w",1,0],["D","w",1,1],["D","w",2,0],["D","w",2,1],["D","bias"],["D","w",3,0],["D","w",3,1],["XT",0],["XT",2],["XE",0],["XT",1],["XQ",0],["XE",2],["XE",1],["Pre"],["XT",3],["XQ",1],["Pq"],["XT",4],["XE",3],["XT",5],["XQ",2],["XE",4],["XQ",3],["WR",0,0],["XE",5],["M1",0],["M1",1],["SQ",0],["M1",2],["M1",3],["SQ",1],["XQ",4],["XT",9],["XQ",5],["WQ",0,0],["SQ",2],["XT",10],["XE",9],["XT",11],["WR",0,1],["XE",10],["TA",0],["XE",11],["SQ",3],["XQ",9],["XT",6],["RT",0],["XQ",10],["XQ",11],["WQ",0,1],["XT",8],["XT",7],["XE",6],["HT",0],["XE",8],["XE",7],["HT",1],["XQ",6],["HE",0],["XQ",8],["XQ",7],["M1",4],["IQ",0],["HE",1],["M1",5],["WR",1,0],["M1",6],["SQ",4],["M1",7],["M1",8],["SQ",5],["M1",9],["HQ"],["M1",10],["SQ",6],["M1",11],["WR",1,1],["M2",0,0],["SQ",7],["TA",1],["SQ",8],["WR",2,0],["SQ",9],["TA",2],["SQ",10],["WR",2,1],["SQ",11],["RT",1],["TA",3],["WQ",1,0],["RT",2],["WQ",1,1],["RT",3],["WQ",2,0],["M2",1,0],["WR",3,0],["WQ",2,1],["WR",3,1],["WQ",3,0],["M2",2,0],["IQ",1],["IQ",2],["M2",0,1],["IQ",3],["BA",0,0],["M2",0,2],["BA",0,1],["SI",0,0],["M2",0,3],["WQ",3,1],["SI",0,1],["ST",0,0],["M2",1,1],["BA",0,2],["M2",1,2],["ST",0,1],["BA",0,3],["SI",0,2],["M2",1,3],["BA",1,0],["M2",2,1],["SI",0,3],["ST",0,2],["BA",1,1],["M2",2,2],["SI",1,0],["ST",0,3],["M2",2,3],["BA",1,2],["SI",1,1],["ST",1,0],["M2",3,0],["BA",1,3],["SI",1,2],["ST",1,1],["M2",3,1],["BA",2,0],["SI",1,3],["ST",1,2],["M2",3,2],["BA",2,1],["SI",2,0],["ST",1,3],["M2",3,3],["BA",2,2],["SI",2,1],["ST",2,0],["BA",2,3],["SI",2,2],["ST",2,1],["BA",3,0],["SI",2,3],["ST",2,2],["BA",3,1],["SI",3,0],["ST",2,3],["BA",3,2],["SI",3,1],["ST",3,0],["BA",3,3],["SI",3,2],["ST",3,1],["SI",3,3],["ST",3,2],["ST",3,3]]
+
+
+def tile_equivariantfeedforward_pa_kernel(tc, h, x1, pre1, w1_0, b1_0, out):
+    nc = tc.nc
+    with ExitStack() as ctx:
+        keep = ctx.enter_context(tc.tile_pool(name="keep", bufs=1))
+        outs = ctx.enter_context(tc.tile_pool(name="outs", bufs=8))
+        psum = ctx.enter_context(tc.psum_pool(name="psum", bufs=8))
+
+        ident_bf = keep.tile([P, P], BF16, name="ident_bf")
+        masks.make_identity(nc, ident_bf[:])
+        ident_f = keep.tile([P, P], F32, name="ident_f")
+        masks.make_identity(nc, ident_f[:])
+        warm = keep.tile([P, 1], F32, name="warm")
+        nc.vector.memset(warm[:], 1.0)
+        warm2 = keep.tile([P, 1], F32, name="warm2")
+        nc.scalar.activation(out=warm2[:], in_=warm[:], func=ACT.Sqrt)
+
+        pre_raw = keep.tile([P, 4, D], BF16, name="pre_raw")
+        x_raw = [keep.tile([P, 4, P, M1], BF16, name="x_raw%d" % i) for i in range(NT)]
+        h_raw = keep.tile([P, NT, D], BF16, name="h_raw")
+        bias = keep.tile([P, F], BF16, name="bias")
+        w_raw = {}
+        w_g = {}
+        for n in range(NF):
+            for g in range(2):
+                w_raw[(n, g)] = keep.tile([P, 4, FC], BF16, name="w_raw%d_%d" % (g, n))
+                w_g[(n, g)] = keep.tile([P, 4 * FC], BF16, name="w_g%d_%d" % (g, n), align_bytes=64)
+        w_c = [keep.tile([P, 2, FC], U32, name="w_c%d" % n, align_bytes=64) for n in range(NF)]
+        w_s = [keep.tile([P, 2, FC], U8, name="w_s%d" % n, align_bytes=64) for n in range(NF)]
+        pre_g = keep.tile([P, 4 * D], BF16, name="pre_g", align_bytes=64)
+        pre_c = keep.tile([P, D], U32, name="pre_c", align_bytes=64)
+        pre_s = keep.tile([P, D], U8, name="pre_s", align_bytes=64)
+        x_g = keep.tile([P, NU * P * 4], BF16, name="x_g", align_bytes=64)
+        x_c = keep.tile([P, NU * P], U32, name="x_c", align_bytes=64)
+        x_s = keep.tile([P, NU * P], U8, name="x_s", align_bytes=64)
+        inv_g = keep.tile([P, NT * P * 4], BF16, name="inv_g", align_bytes=64)
+        inv_c = keep.tile([P, NT * P], U32, name="inv_c", align_bytes=64)
+        inv_s = keep.tile([P, NT * P], U8, name="inv_s", align_bytes=64)
+        h_g = keep.tile([P, NT * P * 4], BF16, name="h_g", align_bytes=64)
+        h_c = keep.tile([P, NT * P], U32, name="h_c", align_bytes=64)
+        h_s = keep.tile([P, NT * P], U8, name="h_s", align_bytes=64)
+        sq = [keep.tile([P, D], F32, name="sq%d" % v) for v in range(NU)]
+        a_c = [h_c, inv_c]
+        a_s = [h_s, inv_s]
+        out_flat = out.rearrange("b n f -> (b n) f")
+        x_rows = x1.rearrange("b n (j q) m -> (b n j) q m", j=4)
+        live = {}
+
+        def load(task):
+            what = task[1]
+            if what == "pre":
+                nc.sync.dma_start(out=pre_raw[:], in_=pre1.rearrange("(j p) e -> p j e", p=P))
+            elif what == "h":
+                nc.sync.dma_start(out=h_raw[:], in_=h.rearrange("b n d -> n b d"))
+            elif what == "bias":
+                nc.sync.dma_start(out=bias[:], in_=b1_0.partition_broadcast(P))
+            elif what == "x":
+                i = task[2]
+                nc.sync.dma_start(
+                    out=x_raw[i][:].rearrange("r a q m -> r a (q m)"),
+                    in_=x_rows[512 * i : 512 * (i + 1), :, :].rearrange("(a r) q m -> r a (q m)", r=P),
+                )
+            else:
+                n, g = task[2], task[3]
+                cols = slice(n * FC, (n + 1) * FC)
+                if g == 0:
+                    for u in range(2):
+                        nc.sync.dma_start(
+                            out=w_raw[(n, 0)][:, 2 * u : 2 * u + 2, :],
+                            in_=w1_0[256 * u : 256 * u + 256, cols].rearrange("(q e) c -> q e c", e=2),
+                        )
+                else:
+                    nc.sync.dma_start(
+                        out=w_raw[(n, 1)][:], in_=w1_0[D : 2 * D, cols].rearrange("(j p) c -> p j c", p=P)
+                    )
+
+        def regroup(eng, dst, src):
+            d = dst.rearrange("p (c i t) -> p c t i", i=4, t=4)
+            s = src.rearrange("p t (c i) -> p c t i", i=4)
+            if eng == "V":
+                nc.vector.tensor_copy(out=d, in_=s)
+            elif eng == "S":
+                nc.scalar.copy(out=d, in_=s)
+            else:
+                nc.gpsimd.tensor_scalar(out=d, in0=s, scalar1=1.0, scalar2=0.0, op0=ALU.mult, op1=ALU.add)
+
+        def leave_psum(eng, dst, src):
+            if eng == "V":
+                nc.vector.tensor_copy(out=dst, in_=src)
+            else:
+                nc.scalar.copy(out=dst, in_=src)
+
+        def quant(codes, scales, src):
+            nc.vector.quantize_mx(out=codes.bitcast(FP8X4), scales=scales, in_=src)
+
+        def xt(v):
+            i, m = divmod(v, M1)
+            t = psum.tile([P, 4, P], BF16, name="xt%d" % v, tag="bank")
+            live[("xt", v)] = t
+            for a in range(4):
+                nc.tensor.transpose(t[:, a, :], x_raw[i][:, a, :, m], ident_bf[:])
+
+        def xe(v):
+            leave_psum(XE[v], x_g[:, 512 * v : 512 * (v + 1)], live[("xt", v)][:].rearrange("p a c -> p (a c)"))
+
+        def xq(v):
+            quant(x_c[:, P * v : P * (v + 1)], x_s[:, P * v : P * (v + 1)], x_g[:, 512 * v : 512 * (v + 1)])
+
+        def m1(v):
+            t = psum.tile([P, D], F32, name="p1_%d" % v, tag="bank")
+            live[("p1", v)] = t
+            nc.tensor.matmul_mx(
+                out=t[:],
+                lhsT=x_c[:, P * v : P * (v + 1)].bitcast(FP8X4),
+                lhsT_scale=x_s[:, P * v : P * (v + 1)],
+                rhs=pre_c[:].bitcast(FP8X4),
+                rhs_scale=pre_s[:],
+                start=True,
+                stop=True,
+            )
+
+        def sqr(v):
+            nc.scalar.activation(out=sq[v][:], in_=live[("p1", v)][:], func=ACT.Square)
+
+        def ta(i):
+            t = psum.tile([P, 4, P], F32, name="acc%d" % i, tag="bank")
+            live[("acc", i)] = t
+            for j in range(4):
+                for m in range(M1):
+                    nc.tensor.matmul(
+                        out=t[:, j, :],
+                        lhsT=sq[M1 * i + m][:, P * j : P * (j + 1)],
+                        rhs=ident_f[:],
+                        is_transpose=True,
+                        start=(m == 0),
+                        stop=(m == M1 - 1),
+                    )
+
+        def rt(i):
+            nc.scalar.activation(
+                out=inv_g[:, 512 * i : 512 * (i + 1)].rearrange("p (t j) -> p t j", j=4),
+                in_=live[("acc", i)][:].rearrange("p j t -> p t j"),
+                func=ACT.Sqrt,
+            )
+
+        def iq(i):
+            quant(inv_c[:, P * i : P * (i + 1)], inv_s[:, P * i : P * (i + 1)], inv_g[:, 512 * i : 512 * (i + 1)])
+
+        def ht(b):
+            t = psum.tile([P, 2, 2, P], F32, name="ht%d" % b, tag="bank")
+            live[("ht", b)] = t
+            for v in range(2):
+                hw = h_raw[:, 2 * b + v, :].bitcast(F32)
+                for u in range(2):
+                    nc.tensor.transpose(t[:, v, u, :], hw[:, P * u : P * (u + 1)], ident_f[:])
+
+        def he(b):
+            leave_psum(
+                HE[b],
+                h_g[:, 1024 * b : 1024 * (b + 1)].bitcast(F32).rearrange("p (v t u) -> p v t u", v=2, u=2),
+                live[("ht", b)][:].rearrange("p v u t -> p v t u"),
+            )
+
+        def m2(n, i):
+            t = psum.tile([P, FC], F32, name="p2_%d_%d" % (n, i), tag="bank")
+            live[("p2", n, i)] = t
+            for g in range(2):
+                nc.tensor.matmul_mx(
+                    out=t[:],
+                    lhsT=a_c[g][:, P * i : P * (i + 1)].bitcast(FP8X4),
+                    lhsT_scale=a_s[g][:, P * i : P * (i + 1)],
+                    rhs=w_c[n][:, g, :].bitcast(FP8X4),
+                    rhs_scale=w_s[n][:, g, :],
+                    start=(g == 0),
+                    stop=(g == 1),
+                )
+
+        def ba(n, i):
+            o = outs.tile([P, FC], F32, name="o")
+            live[("o", n, i)] = o
+            nc.vector.tensor_tensor(
+                out=o[:], in0=live[("p2", n, i)][:], in1=bias[:, n * FC : (n + 1) * FC], op=ALU.add
+            )
+
+        def si(n, i):
+            o = live[("o", n, i)]
+            nc.scalar.activation(out=o[:], in_=o[:], func=ACT.Silu)
+
+        def st(n, i):
+            nc.sync.dma_start(
+                out=out_flat[P * i : P * (i + 1), n * FC : (n + 1) * FC], in_=live[("o", n, i)][:]
+            )
+
+        def run(task):
+            k = task[0]
+            a = task[1:]
+            if k == "D":
+                load(task)
+            elif k == "Pre":
+                regroup(PRE_ENG, pre_g[:], pre_raw[:])
+            elif k == "Pq":
+                quant(pre_c[:], pre_s[:], pre_g[:])
+            elif k == "XT":
+                xt(a[0])
+            elif k == "XE":
+                xe(a[0])
+            elif k == "XQ":
+                xq(a[0])
+            elif k == "M1":
+                m1(a[0])
+            elif k == "SQ":
+                sqr(a[0])
+            elif k == "TA":
+                ta(a[0])
+            elif k == "RT":
+                rt(a[0])
+            elif k == "IQ":
+                iq(a[0])
+            elif k == "HT":
+                ht(a[0])
+            elif k == "HE":
+                he(a[0])
+            elif k == "HQ":
+                quant(h_c[:], h_s[:], h_g[:])
+            elif k == "WR":
+                regroup(WE[a[0]][a[1]], w_g[(a[0], a[1])][:], w_raw[(a[0], a[1])][:])
+            elif k == "WQ":
+                quant(w_c[a[0]][:, a[1], :], w_s[a[0]][:, a[1], :], w_g[(a[0], a[1])][:])
+            elif k == "M2":
+                m2(a[0], a[1])
+            elif k == "BA":
+                ba(a[0], a[1])
+            elif k == "SI":
+                si(a[0], a[1])
+            elif k == "ST":
+                st(a[0], a[1])
+            else:
+                raise ValueError(k)
+
+        if MANUAL:
+            ctx.enter_context(tc.manual_schedule())
+        for task in ORDER:
+            run(task)

@@ -21,12 +21,12 @@ NF = F // FC
 NU = NT * M1
 FLOPS = 2 * (NT * P * M1) * D * D + 2 * (NT * P) * (2 * D) * F
 
-XE = ["V","S","V","S","S","S","V","S","V","S","S","S"]
+XE = ["V","V","S","S","S","V","V","S","S","V","V","S"]
 HE = ["S","S"]
 WE = [["V","V"],["V","V"],["V","V"],["V","S"]]
 PRE_ENG = "V"
 MANUAL = True
-ORDER = [["D","x",0],["D","pre"],["D","x",1],["D","w",0,0],["D","x",3],["D","w",0,1],["D","x",2],["D","h"],["D","w",1,0],["D","w",1,1],["D","w",2,0],["D","w",2,1],["D","bias"],["D","w",3,0],["D","w",3,1],["XT",0],["XT",2],["XE",0],["XT",1],["XQ",0],["XE",2],["XE",1],["Pre"],["XT",3],["XQ",1],["Pq"],["XT",4],["XE",3],["XT",5],["XQ",2],["XE",4],["XQ",3],["WR",0,0],["XE",5],["M1",0],["M1",1],["SQ",0],["M1",2],["M1",3],["SQ",1],["XQ",4],["XT",9],["XQ",5],["WQ",0,0],["SQ",2],["XT",10],["XE",9],["XT",11],["WR",0,1],["XE",10],["TA",0],["XE",11],["SQ",3],["XQ",9],["XT",6],["RT",0],["XQ",10],["XQ",11],["WQ",0,1],["XT",8],["XT",7],["XE",6],["HT",0],["XE",8],["XE",7],["HT",1],["XQ",6],["HE",0],["XQ",8],["XQ",7],["M1",4],["IQ",0],["HE",1],["M1",5],["WR",1,0],["M1",6],["SQ",4],["M1",7],["M1",8],["SQ",5],["M1",9],["HQ"],["M1",10],["SQ",6],["M1",11],["WR",1,1],["M2",0,0],["SQ",7],["TA",1],["SQ",8],["WR",2,0],["SQ",9],["TA",2],["SQ",10],["WR",2,1],["SQ",11],["RT",1],["TA",3],["WQ",1,0],["RT",2],["WQ",1,1],["RT",3],["WQ",2,0],["M2",1,0],["WR",3,0],["WQ",2,1],["WR",3,1],["WQ",3,0],["M2",2,0],["IQ",1],["IQ",2],["M2",0,1],["IQ",3],["BA",0,0],["M2",0,2],["BA",0,1],["SI",0,0],["M2",0,3],["WQ",3,1],["SI",0,1],["ST",0,0],["M2",1,1],["BA",0,2],["M2",1,2],["ST",0,1],["BA",0,3],["SI",0,2],["M2",1,3],["BA",1,0],["M2",2,1],["SI",0,3],["ST",0,2],["BA",1,1],["M2",2,2],["SI",1,0],["ST",0,3],["M2",2,3],["BA",1,2],["SI",1,1],["ST",1,0],["M2",3,0],["BA",1,3],["SI",1,2],["ST",1,1],["M2",3,1],["BA",2,0],["SI",1,3],["ST",1,2],["M2",3,2],["BA",2,1],["SI",2,0],["ST",1,3],["M2",3,3],["BA",2,2],["SI",2,1],["ST",2,0],["BA",2,3],["SI",2,2],["ST",2,1],["BA",3,0],["SI",2,3],["ST",2,2],["BA",3,1],["SI",3,0],["ST",2,3],["BA",3,2],["SI",3,1],["ST",3,0],["BA",3,3],["SI",3,2],["ST",3,1],["SI",3,3],["ST",3,2],["ST",3,3]]
+ORDER = [["D","x",0],["D","pre"],["D","x",1],["D","w",0,1],["D","x",2],["D","w",0,0],["D","x",3],["D","w",1,1],["D","bias"],["D","w",1,0],["D","h"],["D","w",2,1],["D","w",2,0],["D","w",3,1],["D","w",3,0],["DW",0],["DW",1],["DW",2],["DW",3],["DW",4],["DW",5],["DW",6],["XT",0],["XT",1],["XE",0],["XT",2],["XQ",0],["XE",1],["DK",0],["XE",2],["Pre"],["XT",3],["XQ",1],["Pq"],["XT",4],["XE",3],["XT",5],["XQ",2],["XE",4],["XQ",3],["WR",0,1],["M1",0],["M1",1],["SQ",0],["M1",2],["SQ",1],["XT",6],["XE",5],["XQ",4],["XT",7],["SQ",2],["XE",6],["XT",8],["XQ",5],["XE",7],["XQ",6],["WQ",0,1],["XE",8],["M1",3],["M1",4],["SQ",3],["XQ",7],["M1",5],["XQ",8],["WR",0,0],["SQ",4],["TA",0],["SQ",5],["WQ",0,0],["M1",6],["RT",0],["M1",7],["WR",1,1],["M1",8],["SQ",6],["XT",9],["SQ",7],["XT",10],["XE",9],["SQ",8],["XT",11],["XE",10],["DK",1],["XE",11],["XQ",9],["TA",1],["XQ",10],["WQ",1,1],["XQ",11],["WR",1,0],["RT",1],["M1",9],["M1",10],["M1",11],["SQ",9],["TA",2],["IQ",0],["WQ",1,0],["SQ",10],["SQ",11],["IQ",1],["WR",2,1],["HT",0],["HT",1],["RT",2],["HE",0],["IQ",2],["WR",2,0],["HE",1],["HQ"],["WR",3,1],["WQ",2,0],["MA",0,0],["MA",0,1],["WQ",2,1],["MA",0,2],["MA",0,3],["WR",3,0],["TA",3],["WQ",3,1],["RT",3],["MB",0,0],["MB",0,1],["WQ",3,0],["MB",0,2],["IQ",3],["BA",0,0],["MB",0,3],["MA",1,0],["BA",0,1],["MB",1,0],["MA",1,1],["SI",0,0],["BA",0,2],["MB",1,1],["MA",1,2],["SI",0,1],["BA",0,3],["ST",0,0],["MB",1,2],["SI",0,2],["MA",1,3],["BA",1,0],["ST",0,1],["MB",1,3],["SI",0,3],["MA",2,0],["BA",1,1],["ST",0,2],["MB",2,0],["SI",1,0],["BA",1,2],["MA",2,1],["ST",0,3],["SI",1,1],["MB",2,1],["BA",1,3],["MA",2,2],["ST",1,0],["SI",1,2],["MB",2,2],["BA",2,0],["ST",1,1],["MA",2,3],["SI",1,3],["MB",2,3],["BA",2,1],["ST",1,2],["MA",3,0],["SI",2,0],["MB",3,0],["BA",2,2],["ST",1,3],["SI",2,1],["MA",3,1],["MB",3,1],["BA",2,3],["ST",2,0],["SI",2,2],["MA",3,2],["BA",3,0],["MB",3,2],["SI",2,3],["ST",2,1],["MA",3,3],["BA",3,1],["MB",3,3],["SI",3,0],["ST",2,2],["BA",3,2],["SI",3,1],["ST",2,3],["BA",3,3],["SI",3,2],["ST",3,0],["SI",3,3],["ST",3,1],["ST",3,2],["ST",3,3]]
 
 
 def tile_equivariantfeedforward_pa_kernel(tc, h, x1, pre1, w1_0, b1_0, out):
@@ -45,6 +45,11 @@ def tile_equivariantfeedforward_pa_kernel(tc, h, x1, pre1, w1_0, b1_0, out):
         warm2 = keep.tile([P, 1], F32, name="warm2")
         nc.scalar.activation(out=warm2[:], in_=warm[:], func=ACT.Sqrt)
 
+        zero_b = keep.tile([P, 4 * D], BF16, name="zero_b", align_bytes=64)
+        nc.vector.memset(zero_b[:], 0.0)
+        zero_c = keep.tile([P, D], U32, name="zero_c", align_bytes=64)
+        zero_s = keep.tile([P, D], U8, name="zero_s", align_bytes=64)
+        nc.vector.quantize_mx(out=zero_c[:].bitcast(FP8X4), scales=zero_s[:], in_=zero_b[:])
         pre_raw = keep.tile([P, 4, D], BF16, name="pre_raw")
         x_raw = [keep.tile([P, 4, P, M1], BF16, name="x_raw%d" % i) for i in range(NT)]
         h_raw = keep.tile([P, NT, D], BF16, name="h_raw")
@@ -191,19 +196,39 @@ def tile_equivariantfeedforward_pa_kernel(tc, h, x1, pre1, w1_0, b1_0, out):
                 live[("ht", b)][:].rearrange("p v u t -> p v t u"),
             )
 
-        def m2(n, i):
-            t = psum.tile([P, FC], F32, name="p2_%d_%d" % (n, i), tag="bank")
-            live[("p2", n, i)] = t
-            for g in range(2):
-                nc.tensor.matmul_mx(
-                    out=t[:],
-                    lhsT=a_c[g][:, P * i : P * (i + 1)].bitcast(FP8X4),
-                    lhsT_scale=a_s[g][:, P * i : P * (i + 1)],
-                    rhs=w_c[n][:, g, :].bitcast(FP8X4),
-                    rhs_scale=w_s[n][:, g, :],
-                    start=(g == 0),
-                    stop=(g == 1),
-                )
+        def dummy_bank():
+            if "dmy" not in live:
+                dmy = psum.tile([P, D], F32, name="dmy", tag="bank")
+                live["dmy"] = dmy
+            return live["dmy"]
+
+        def dw():
+            nc.tensor.matmul_mx(
+                out=dummy_bank()[:],
+                lhsT=zero_c[:, 0:P].bitcast(FP8X4),
+                lhsT_scale=zero_s[:, 0:P],
+                rhs=zero_c[:].bitcast(FP8X4),
+                rhs_scale=zero_s[:],
+                start=True,
+                stop=True,
+            )
+
+        def dk():
+            nc.tensor.matmul(out=dummy_bank()[:], lhsT=zero_b[:, 0:P], rhs=zero_b[:, 0:D], start=True, stop=True)
+
+        def m2(n, i, g):
+            if g == 0:
+                t = psum.tile([P, FC], F32, name="p2_%d_%d" % (n, i), tag="bank")
+                live[("p2", n, i)] = t
+            nc.tensor.matmul_mx(
+                out=live[("p2", n, i)][:],
+                lhsT=a_c[g][:, P * i : P * (i + 1)].bitcast(FP8X4),
+                lhsT_scale=a_s[g][:, P * i : P * (i + 1)],
+                rhs=w_c[n][:, g, :].bitcast(FP8X4),
+                rhs_scale=w_s[n][:, g, :],
+                start=(g == 0),
+                stop=(g == 1),
+            )
 
         def ba(n, i):
             o = outs.tile([P, FC], F32, name="o")
@@ -256,8 +281,14 @@ def tile_equivariantfeedforward_pa_kernel(tc, h, x1, pre1, w1_0, b1_0, out):
                 regroup(WE[a[0]][a[1]], w_g[(a[0], a[1])][:], w_raw[(a[0], a[1])][:])
             elif k == "WQ":
                 quant(w_c[a[0]][:, a[1], :], w_s[a[0]][:, a[1], :], w_g[(a[0], a[1])][:])
-            elif k == "M2":
-                m2(a[0], a[1])
+            elif k == "MA":
+                m2(a[0], a[1], 0)
+            elif k == "MB":
+                m2(a[0], a[1], 1)
+            elif k == "DW":
+                dw()
+            elif k == "DK":
+                dk()
             elif k == "BA":
                 ba(a[0], a[1])
             elif k == "SI":

@@ -21,12 +21,13 @@ NF = F // FC
 NU = NT * M1
 FLOPS = 2 * (NT * P * M1) * D * D + 2 * (NT * P) * (2 * D) * F
 
-XE = ["V","V","S","S","S","V","V","S","S","V","V","S"]
+XE = ["V","S","V","S","S","S","V","S","V","S","S","S"]
 HE = ["S","S"]
 WE = [["V","V"],["V","V"],["V","V"],["V","S"]]
+BE = ["S","S","S","S"]
 PRE_ENG = "V"
 MANUAL = True
-ORDER = [["D","x",0],["D","pre"],["D","x",1],["D","w",0,1],["D","x",2],["D","w",0,0],["D","x",3],["D","w",1,1],["D","bias"],["D","w",1,0],["D","h"],["D","w",2,1],["D","w",2,0],["D","w",3,1],["D","w",3,0],["DW",0],["DW",1],["DW",2],["DW",3],["DW",4],["DW",5],["DW",6],["XT",0],["XT",1],["XE",0],["XT",2],["XQ",0],["XE",1],["DK",0],["XE",2],["Pre"],["XT",3],["XQ",1],["Pq"],["XT",4],["XE",3],["XT",5],["XQ",2],["XE",4],["XQ",3],["WR",0,1],["M1",0],["M1",1],["SQ",0],["M1",2],["SQ",1],["XT",6],["XE",5],["XQ",4],["XT",7],["SQ",2],["XE",6],["XT",8],["XQ",5],["XE",7],["XQ",6],["WQ",0,1],["XE",8],["M1",3],["M1",4],["SQ",3],["XQ",7],["M1",5],["XQ",8],["WR",0,0],["SQ",4],["TA",0],["SQ",5],["WQ",0,0],["M1",6],["RT",0],["M1",7],["WR",1,1],["M1",8],["SQ",6],["XT",9],["SQ",7],["XT",10],["XE",9],["SQ",8],["XT",11],["XE",10],["DK",1],["XE",11],["XQ",9],["TA",1],["XQ",10],["WQ",1,1],["XQ",11],["WR",1,0],["RT",1],["M1",9],["M1",10],["M1",11],["SQ",9],["TA",2],["IQ",0],["WQ",1,0],["SQ",10],["SQ",11],["IQ",1],["WR",2,1],["HT",0],["HT",1],["RT",2],["HE",0],["IQ",2],["WR",2,0],["HE",1],["HQ"],["WR",3,1],["WQ",2,0],["MA",0,0],["MA",0,1],["WQ",2,1],["MA",0,2],["MA",0,3],["WR",3,0],["TA",3],["WQ",3,1],["RT",3],["MB",0,0],["MB",0,1],["WQ",3,0],["MB",0,2],["IQ",3],["BA",0,0],["MB",0,3],["MA",1,0],["BA",0,1],["MB",1,0],["MA",1,1],["SI",0,0],["BA",0,2],["MB",1,1],["MA",1,2],["SI",0,1],["BA",0,3],["ST",0,0],["MB",1,2],["SI",0,2],["MA",1,3],["BA",1,0],["ST",0,1],["MB",1,3],["SI",0,3],["MA",2,0],["BA",1,1],["ST",0,2],["MB",2,0],["SI",1,0],["BA",1,2],["MA",2,1],["ST",0,3],["SI",1,1],["MB",2,1],["BA",1,3],["MA",2,2],["ST",1,0],["SI",1,2],["MB",2,2],["BA",2,0],["ST",1,1],["MA",2,3],["SI",1,3],["MB",2,3],["BA",2,1],["ST",1,2],["MA",3,0],["SI",2,0],["MB",3,0],["BA",2,2],["ST",1,3],["SI",2,1],["MA",3,1],["MB",3,1],["BA",2,3],["ST",2,0],["SI",2,2],["MA",3,2],["BA",3,0],["MB",3,2],["SI",2,3],["ST",2,1],["MA",3,3],["BA",3,1],["MB",3,3],["SI",3,0],["ST",2,2],["BA",3,2],["SI",3,1],["ST",2,3],["BA",3,3],["SI",3,2],["ST",3,0],["SI",3,3],["ST",3,1],["ST",3,2],["ST",3,3]]
+ORDER = [["D","bias"],["D","x",0],["D","pre"],["D","x",1],["D","w",0,0],["D","x",3],["D","w",0,1],["D","x",2],["D","h"],["D","w",1,0],["D","w",1,1],["D","w",2,0],["D","w",2,1],["D","w",3,0],["D","w",3,1],["BB",0],["BB",1],["BE",0],["BB",2],["BE",1],["BB",3],["BE",2],["BE",3],["XT",0],["XT",2],["XE",0],["XT",1],["XQ",0],["XE",2],["XE",1],["Pre"],["XT",3],["XQ",1],["Pq"],["XT",4],["XE",3],["XT",5],["XQ",2],["XE",4],["XQ",3],["WR",0,0],["XE",5],["M1",0],["M1",1],["SQ",0],["M1",2],["M1",3],["SQ",1],["XQ",4],["XT",9],["XQ",5],["WQ",0,0],["SQ",2],["XT",10],["XE",9],["XT",11],["WR",0,1],["XE",10],["TA",0],["XE",11],["SQ",3],["XQ",9],["XT",6],["RT",0],["XQ",10],["XQ",11],["WQ",0,1],["XT",8],["XT",7],["XE",6],["HT",0],["XE",8],["XE",7],["HT",1],["XQ",6],["HE",0],["XQ",8],["XQ",7],["M1",4],["IQ",0],["HE",1],["M1",5],["WR",1,0],["M1",6],["SQ",4],["M1",7],["M1",8],["SQ",5],["M1",9],["HQ"],["M1",10],["SQ",6],["M1",11],["WR",1,1],["M2",0,0],["SQ",7],["TA",1],["SQ",8],["WR",2,0],["SQ",9],["TA",2],["SQ",10],["WR",2,1],["SQ",11],["RT",1],["TA",3],["WQ",1,0],["RT",2],["WQ",1,1],["RT",3],["WQ",2,0],["M2",1,0],["WR",3,0],["WQ",2,1],["WR",3,1],["WQ",3,0],["M2",2,0],["IQ",1],["IQ",2],["M2",0,1],["IQ",3],["BA",0,0],["M2",0,2],["BA",0,1],["SI",0,0],["M2",0,3],["WQ",3,1],["SI",0,1],["ST",0,0],["M2",1,1],["BA",0,2],["M2",1,2],["ST",0,1],["BA",0,3],["SI",0,2],["M2",1,3],["BA",1,0],["M2",2,1],["SI",0,3],["ST",0,2],["BA",1,1],["M2",2,2],["SI",1,0],["ST",0,3],["M2",2,3],["BA",1,2],["SI",1,1],["ST",1,0],["M2",3,0],["BA",1,3],["SI",1,2],["ST",1,1],["M2",3,1],["BA",2,0],["SI",1,3],["ST",1,2],["M2",3,2],["BA",2,1],["SI",2,0],["ST",1,3],["M2",3,3],["BA",2,2],["SI",2,1],["ST",2,0],["BA",2,3],["SI",2,2],["ST",2,1],["BA",3,0],["SI",2,3],["ST",2,2],["BA",3,1],["SI",3,0],["ST",2,3],["BA",3,2],["SI",3,1],["ST",3,0],["BA",3,3],["SI",3,2],["ST",3,1],["SI",3,3],["ST",3,2],["ST",3,3]]
 
 
 def tile_equivariantfeedforward_pa_kernel(tc, h, x1, pre1, w1_0, b1_0, out):
@@ -45,15 +46,14 @@ def tile_equivariantfeedforward_pa_kernel(tc, h, x1, pre1, w1_0, b1_0, out):
         warm2 = keep.tile([P, 1], F32, name="warm2")
         nc.scalar.activation(out=warm2[:], in_=warm[:], func=ACT.Sqrt)
 
-        zero_b = keep.tile([P, 4 * D], BF16, name="zero_b", align_bytes=64)
-        nc.vector.memset(zero_b[:], 0.0)
-        zero_c = keep.tile([P, D], U32, name="zero_c", align_bytes=64)
-        zero_s = keep.tile([P, D], U8, name="zero_s", align_bytes=64)
-        nc.vector.quantize_mx(out=zero_c[:].bitcast(FP8X4), scales=zero_s[:], in_=zero_b[:])
         pre_raw = keep.tile([P, 4, D], BF16, name="pre_raw")
         x_raw = [keep.tile([P, 4, P, M1], BF16, name="x_raw%d" % i) for i in range(NT)]
         h_raw = keep.tile([P, NT, D], BF16, name="h_raw")
-        bias = keep.tile([P, F], BF16, name="bias")
+        bias = keep.tile([P, F], F32, name="bias")
+        b_row = keep.tile([P, F], BF16, name="b_row")
+        nc.vector.memset(b_row[:].bitcast(mybir.dt.int32), 0)
+        ones = keep.tile([P, P], BF16, name="ones")
+        nc.vector.memset(ones[:], 1.0)
         w_raw = {}
         w_g = {}
         for n in range(NF):
@@ -88,7 +88,7 @@ def tile_equivariantfeedforward_pa_kernel(tc, h, x1, pre1, w1_0, b1_0, out):
             elif what == "h":
                 nc.sync.dma_start(out=h_raw[:], in_=h.rearrange("b n d -> n b d"))
             elif what == "bias":
-                nc.sync.dma_start(out=bias[:], in_=b1_0.partition_broadcast(P))
+                nc.sync.dma_start(out=b_row[0:1, :], in_=b1_0.unsqueeze(0))
             elif what == "x":
                 i = task[2]
                 nc.sync.dma_start(
@@ -196,39 +196,19 @@ def tile_equivariantfeedforward_pa_kernel(tc, h, x1, pre1, w1_0, b1_0, out):
                 live[("ht", b)][:].rearrange("p v u t -> p v t u"),
             )
 
-        def dummy_bank():
-            if "dmy" not in live:
-                dmy = psum.tile([P, D], F32, name="dmy", tag="bank")
-                live["dmy"] = dmy
-            return live["dmy"]
-
-        def dw():
-            nc.tensor.matmul_mx(
-                out=dummy_bank()[:],
-                lhsT=zero_c[:, 0:P].bitcast(FP8X4),
-                lhsT_scale=zero_s[:, 0:P],
-                rhs=zero_c[:].bitcast(FP8X4),
-                rhs_scale=zero_s[:],
-                start=True,
-                stop=True,
-            )
-
-        def dk():
-            nc.tensor.matmul(out=dummy_bank()[:], lhsT=zero_b[:, 0:P], rhs=zero_b[:, 0:D], start=True, stop=True)
-
-        def m2(n, i, g):
-            if g == 0:
-                t = psum.tile([P, FC], F32, name="p2_%d_%d" % (n, i), tag="bank")
-                live[("p2", n, i)] = t
-            nc.tensor.matmul_mx(
-                out=live[("p2", n, i)][:],
-                lhsT=a_c[g][:, P * i : P * (i + 1)].bitcast(FP8X4),
-                lhsT_scale=a_s[g][:, P * i : P * (i + 1)],
-                rhs=w_c[n][:, g, :].bitcast(FP8X4),
-                rhs_scale=w_s[n][:, g, :],
-                start=(g == 0),
-                stop=(g == 1),
-            )
+        def m2(n, i):
+            t = psum.tile([P, FC], F32, name="p2_%d_%d" % (n, i), tag="bank")
+            live[("p2", n, i)] = t
+            for g in range(2):
+                nc.tensor.matmul_mx(
+                    out=t[:],
+                    lhsT=a_c[g][:, P * i : P * (i + 1)].bitcast(FP8X4),
+                    lhsT_scale=a_s[g][:, P * i : P * (i + 1)],
+                    rhs=w_c[n][:, g, :].bitcast(FP8X4),
+                    rhs_scale=w_s[n][:, g, :],
+                    start=(g == 0),
+                    stop=(g == 1),
+                )
 
         def ba(n, i):
             o = outs.tile([P, FC], F32, name="o")
@@ -245,6 +225,14 @@ def tile_equivariantfeedforward_pa_kernel(tc, h, x1, pre1, w1_0, b1_0, out):
             nc.sync.dma_start(
                 out=out_flat[P * i : P * (i + 1), n * FC : (n + 1) * FC], in_=live[("o", n, i)][:]
             )
+
+        def bb(n):
+            t = psum.tile([P, FC], F32, name="bb%d" % n, tag="bank")
+            live[("bb", n)] = t
+            nc.tensor.matmul(out=t[:], lhsT=ones[:], rhs=b_row[:, n * FC : (n + 1) * FC], start=True, stop=True)
+
+        def be(n):
+            leave_psum(BE[n], bias[:, n * FC : (n + 1) * FC], live[("bb", n)][:])
 
         def run(task):
             k = task[0]
@@ -281,14 +269,12 @@ def tile_equivariantfeedforward_pa_kernel(tc, h, x1, pre1, w1_0, b1_0, out):
                 regroup(WE[a[0]][a[1]], w_g[(a[0], a[1])][:], w_raw[(a[0], a[1])][:])
             elif k == "WQ":
                 quant(w_c[a[0]][:, a[1], :], w_s[a[0]][:, a[1], :], w_g[(a[0], a[1])][:])
-            elif k == "MA":
-                m2(a[0], a[1], 0)
-            elif k == "MB":
-                m2(a[0], a[1], 1)
-            elif k == "DW":
-                dw()
-            elif k == "DK":
-                dk()
+            elif k == "BB":
+                bb(a[0])
+            elif k == "BE":
+                be(a[0])
+            elif k == "M2":
+                m2(a[0], a[1])
             elif k == "BA":
                 ba(a[0], a[1])
             elif k == "SI":

@@ -24,10 +24,10 @@ FLOPS = 2 * (NT * P * M1) * D * D + 2 * (NT * P) * (2 * D) * F
 XE = ["V","S","V","S","S","S","V","S","V","S","S","S"]
 HE = ["S","S"]
 WE = [["V","V"],["V","V"],["V","V"],["V","S"]]
-BE = ["S","S","S","S"]
+BE = ["S","S"]
 PRE_ENG = "V"
 MANUAL = True
-ORDER = [["D","bias"],["D","x",0],["D","pre"],["D","x",1],["D","w",0,0],["D","x",3],["D","w",0,1],["D","x",2],["D","h"],["D","w",1,0],["D","w",1,1],["D","w",2,0],["D","w",2,1],["D","w",3,0],["D","w",3,1],["BB",0],["BB",1],["BE",0],["BB",2],["BE",1],["BB",3],["BE",2],["BE",3],["XT",0],["XT",2],["XE",0],["XT",1],["XQ",0],["XE",2],["XE",1],["Pre"],["XT",3],["XQ",1],["Pq"],["XT",4],["XE",3],["XT",5],["XQ",2],["XE",4],["XQ",3],["WR",0,0],["XE",5],["M1",0],["M1",1],["SQ",0],["M1",2],["M1",3],["SQ",1],["XQ",4],["XT",9],["XQ",5],["WQ",0,0],["SQ",2],["XT",10],["XE",9],["XT",11],["WR",0,1],["XE",10],["TA",0],["XE",11],["SQ",3],["XQ",9],["XT",6],["RT",0],["XQ",10],["XQ",11],["WQ",0,1],["XT",8],["XT",7],["XE",6],["HT",0],["XE",8],["XE",7],["HT",1],["XQ",6],["HE",0],["XQ",8],["XQ",7],["M1",4],["IQ",0],["HE",1],["M1",5],["WR",1,0],["M1",6],["SQ",4],["M1",7],["M1",8],["SQ",5],["M1",9],["HQ"],["M1",10],["SQ",6],["M1",11],["WR",1,1],["M2",0,0],["SQ",7],["TA",1],["SQ",8],["WR",2,0],["SQ",9],["TA",2],["SQ",10],["WR",2,1],["SQ",11],["RT",1],["TA",3],["WQ",1,0],["RT",2],["WQ",1,1],["RT",3],["WQ",2,0],["M2",1,0],["WR",3,0],["WQ",2,1],["WR",3,1],["WQ",3,0],["M2",2,0],["IQ",1],["IQ",2],["M2",0,1],["IQ",3],["BA",0,0],["M2",0,2],["BA",0,1],["SI",0,0],["M2",0,3],["WQ",3,1],["SI",0,1],["ST",0,0],["M2",1,1],["BA",0,2],["M2",1,2],["ST",0,1],["BA",0,3],["SI",0,2],["M2",1,3],["BA",1,0],["M2",2,1],["SI",0,3],["ST",0,2],["BA",1,1],["M2",2,2],["SI",1,0],["ST",0,3],["M2",2,3],["BA",1,2],["SI",1,1],["ST",1,0],["M2",3,0],["BA",1,3],["SI",1,2],["ST",1,1],["M2",3,1],["BA",2,0],["SI",1,3],["ST",1,2],["M2",3,2],["BA",2,1],["SI",2,0],["ST",1,3],["M2",3,3],["BA",2,2],["SI",2,1],["ST",2,0],["BA",2,3],["SI",2,2],["ST",2,1],["BA",3,0],["SI",2,3],["ST",2,2],["BA",3,1],["SI",3,0],["ST",2,3],["BA",3,2],["SI",3,1],["ST",3,0],["BA",3,3],["SI",3,2],["ST",3,1],["SI",3,3],["ST",3,2],["ST",3,3]]
+ORDER = [["D","x",0],["D","bias"],["D","pre"],["D","x",1],["D","w",0,0],["D","x",3],["D","w",0,1],["D","x",2],["D","h"],["D","w",1,0],["D","w",1,1],["D","w",2,0],["D","w",2,1],["D","w",3,0],["D","w",3,1],["XT",0],["XT",2],["XE",0],["XT",1],["XQ",0],["XE",2],["BB",0],["XE",1],["Pre"],["BB",1],["BE",0],["XT",3],["XQ",1],["BE",1],["Pq"],["XT",4],["XE",3],["XQ",2],["XT",5],["XE",4],["XQ",3],["WR",0,0],["XE",5],["M1",0],["M1",1],["SQ",0],["M1",2],["M1",3],["SQ",1],["XQ",4],["XQ",5],["XT",9],["WQ",0,0],["SQ",2],["XT",10],["XE",9],["XT",11],["WR",0,1],["XE",10],["TA",0],["XE",11],["SQ",3],["XQ",9],["XT",6],["XQ",10],["RT",0],["XQ",11],["WQ",0,1],["XT",8],["XT",7],["XE",6],["XE",8],["HT",0],["XE",7],["XQ",6],["HT",1],["HE",0],["XQ",8],["XQ",7],["IQ",0],["M1",4],["HE",1],["M1",5],["WR",1,0],["M1",6],["SQ",4],["M1",7],["M1",8],["SQ",5],["M1",9],["HQ"],["M1",10],["SQ",6],["M1",11],["WR",1,1],["M2",0,0],["SQ",7],["TA",1],["SQ",8],["WR",2,0],["SQ",9],["TA",2],["SQ",10],["WR",2,1],["SQ",11],["RT",1],["TA",3],["WQ",1,0],["RT",2],["WQ",1,1],["RT",3],["WQ",2,0],["M2",1,0],["WR",3,0],["WQ",2,1],["WR",3,1],["WQ",3,0],["M2",2,0],["IQ",1],["IQ",2],["M2",0,1],["IQ",3],["BA",0,0],["M2",0,2],["BA",0,1],["SI",0,0],["M2",0,3],["WQ",3,1],["SI",0,1],["M2",1,1],["ST",0,0],["BA",0,2],["M2",1,2],["ST",0,1],["BA",0,3],["SI",0,2],["M2",1,3],["BA",1,0],["M2",2,1],["SI",0,3],["ST",0,2],["BA",1,1],["M2",2,2],["SI",1,0],["ST",0,3],["M2",2,3],["BA",1,2],["SI",1,1],["ST",1,0],["M2",3,0],["BA",1,3],["SI",1,2],["ST",1,1],["M2",3,1],["BA",2,0],["SI",1,3],["ST",1,2],["M2",3,2],["BA",2,1],["SI",2,0],["ST",1,3],["M2",3,3],["BA",2,2],["SI",2,1],["ST",2,0],["BA",2,3],["SI",2,2],["ST",2,1],["BA",3,0],["SI",2,3],["ST",2,2],["BA",3,1],["SI",3,0],["ST",2,3],["BA",3,2],["SI",3,1],["ST",3,0],["BA",3,3],["SI",3,2],["ST",3,1],["SI",3,3],["ST",3,2],["ST",3,3]]
 
 
 def tile_equivariantfeedforward_pa_kernel(tc, h, x1, pre1, w1_0, b1_0, out):
@@ -49,7 +49,7 @@ def tile_equivariantfeedforward_pa_kernel(tc, h, x1, pre1, w1_0, b1_0, out):
         pre_raw = keep.tile([P, 4, D], BF16, name="pre_raw")
         x_raw = [keep.tile([P, 4, P, M1], BF16, name="x_raw%d" % i) for i in range(NT)]
         h_raw = keep.tile([P, NT, D], BF16, name="h_raw")
-        bias = keep.tile([P, F], F32, name="bias")
+        bias = keep.tile([P, F], BF16, name="bias")
         b_row = keep.tile([P, F], BF16, name="b_row")
         nc.vector.memset(b_row[:].bitcast(mybir.dt.int32), 0)
         ones = keep.tile([P, P], BF16, name="ones")
@@ -117,7 +117,16 @@ def tile_equivariantfeedforward_pa_kernel(tc, h, x1, pre1, w1_0, b1_0, out):
             elif eng == "S":
                 nc.scalar.copy(out=d, in_=s)
             else:
-                nc.gpsimd.tensor_scalar(out=d, in0=s, scalar1=1.0, scalar2=0.0, op0=ALU.mult, op1=ALU.add)
+                half = d.shape[1] // 2
+                for q in range(2):
+                    nc.gpsimd.tensor_scalar(
+                        out=d[:, q * half : (q + 1) * half, :, :],
+                        in0=s[:, q * half : (q + 1) * half, :, :],
+                        scalar1=1.0,
+                        scalar2=0.0,
+                        op0=ALU.mult,
+                        op1=ALU.add,
+                    )
 
         def leave_psum(eng, dst, src):
             if eng == "V":
@@ -226,13 +235,20 @@ def tile_equivariantfeedforward_pa_kernel(tc, h, x1, pre1, w1_0, b1_0, out):
                 out=out_flat[P * i : P * (i + 1), n * FC : (n + 1) * FC], in_=live[("o", n, i)][:]
             )
 
-        def bb(n):
-            t = psum.tile([P, FC], F32, name="bb%d" % n, tag="bank")
-            live[("bb", n)] = t
-            nc.tensor.matmul(out=t[:], lhsT=ones[:], rhs=b_row[:, n * FC : (n + 1) * FC], start=True, stop=True)
+        def bb(c):
+            t = psum.tile([P, 2 * FC], BF16, name="bb%d" % c, tag="bank")
+            live[("bb", c)] = t
+            for n in range(2):
+                nc.tensor.matmul(
+                    out=t[:, n * FC : (n + 1) * FC],
+                    lhsT=ones[:],
+                    rhs=b_row[:, (2 * c + n) * FC : (2 * c + n + 1) * FC],
+                    start=True,
+                    stop=True,
+                )
 
-        def be(n):
-            leave_psum(BE[n], bias[:, n * FC : (n + 1) * FC], live[("bb", n)][:])
+        def be(c):
+            leave_psum(BE[c], bias[:, 2 * c * FC : 2 * (c + 1) * FC], live[("bb", c)][:])
 
         def run(task):
             k = task[0]

@@ -21,13 +21,12 @@ NF = F // FC
 NU = NT * M1
 FLOPS = 2 * (NT * P * M1) * D * D + 2 * (NT * P) * (2 * D) * F
 
-XE = ["V","S","V","S","S","S","V","S","V","S","S","S"]
+XE = ["S","S","S","S","S","S","S","S","S","S","S","S"]
 HE = ["S","S"]
-WE = [["V","V"],["V","V"],["V","V"],["V","S"]]
-BE = ["S","S"]
+WE = [["V","V"],["V","V"],["V","V"],["G","G"]]
 PRE_ENG = "V"
 MANUAL = True
-ORDER = [["D","x",0],["D","bias"],["D","pre"],["D","x",1],["D","w",0,0],["D","x",3],["D","w",0,1],["D","x",2],["D","h"],["D","w",1,0],["D","w",1,1],["D","w",2,0],["D","w",2,1],["D","w",3,0],["D","w",3,1],["XT",0],["XT",2],["XE",0],["XT",1],["XQ",0],["XE",2],["BB",0],["XE",1],["Pre"],["BB",1],["BE",0],["XT",3],["XQ",1],["BE",1],["Pq"],["XT",4],["XE",3],["XQ",2],["XT",5],["XE",4],["XQ",3],["WR",0,0],["XE",5],["M1",0],["M1",1],["SQ",0],["M1",2],["M1",3],["SQ",1],["XQ",4],["XQ",5],["XT",9],["WQ",0,0],["SQ",2],["XT",10],["XE",9],["XT",11],["WR",0,1],["XE",10],["TA",0],["XE",11],["SQ",3],["XQ",9],["XT",6],["XQ",10],["RT",0],["XQ",11],["WQ",0,1],["XT",8],["XT",7],["XE",6],["XE",8],["HT",0],["XE",7],["XQ",6],["HT",1],["HE",0],["XQ",8],["XQ",7],["IQ",0],["M1",4],["HE",1],["M1",5],["WR",1,0],["M1",6],["SQ",4],["M1",7],["M1",8],["SQ",5],["M1",9],["HQ"],["M1",10],["SQ",6],["M1",11],["WR",1,1],["M2",0,0],["SQ",7],["TA",1],["SQ",8],["WR",2,0],["SQ",9],["TA",2],["SQ",10],["WR",2,1],["SQ",11],["RT",1],["TA",3],["WQ",1,0],["RT",2],["WQ",1,1],["RT",3],["WQ",2,0],["M2",1,0],["WR",3,0],["WQ",2,1],["WR",3,1],["WQ",3,0],["M2",2,0],["IQ",1],["IQ",2],["M2",0,1],["IQ",3],["BA",0,0],["M2",0,2],["BA",0,1],["SI",0,0],["M2",0,3],["WQ",3,1],["SI",0,1],["M2",1,1],["ST",0,0],["BA",0,2],["M2",1,2],["ST",0,1],["BA",0,3],["SI",0,2],["M2",1,3],["BA",1,0],["M2",2,1],["SI",0,3],["ST",0,2],["BA",1,1],["M2",2,2],["SI",1,0],["ST",0,3],["M2",2,3],["BA",1,2],["SI",1,1],["ST",1,0],["M2",3,0],["BA",1,3],["SI",1,2],["ST",1,1],["M2",3,1],["BA",2,0],["SI",1,3],["ST",1,2],["M2",3,2],["BA",2,1],["SI",2,0],["ST",1,3],["M2",3,3],["BA",2,2],["SI",2,1],["ST",2,0],["BA",2,3],["SI",2,2],["ST",2,1],["BA",3,0],["SI",2,3],["ST",2,2],["BA",3,1],["SI",3,0],["ST",2,3],["BA",3,2],["SI",3,1],["ST",3,0],["BA",3,3],["SI",3,2],["ST",3,1],["SI",3,3],["ST",3,2],["ST",3,3]]
+ORDER = [["D","x",0],["D","pre"],["D","x",1],["D","w",0,0],["D","x",3],["D","w",0,1],["D","x",2],["D","h"],["D","w",1,0],["D","w",1,1],["D","w",2,0],["D","w",2,1],["D","bias"],["D","w",3,0],["D","w",3,1],["XT",0],["XT",2],["XE",0],["XT",1],["XQ",0],["XE",2],["Pre"],["XE",1],["XT",3],["XQ",1],["Pq"],["XT",4],["XE",3],["XQ",2],["XT",5],["XE",4],["XQ",3],["WR",0,0],["XE",5],["M1",0],["M1",1],["SQ",0],["M1",2],["M1",3],["SQ",1],["XQ",4],["XT",9],["XQ",5],["WQ",0,0],["SQ",2],["XT",10],["XE",9],["XT",11],["WR",0,1],["XE",10],["TA",0],["XE",11],["SQ",3],["XQ",9],["XT",6],["RT",0],["XQ",10],["XQ",11],["XT",8],["WQ",0,1],["XE",6],["XT",7],["XE",8],["XQ",6],["HT",0],["XE",7],["XQ",8],["HT",1],["HE",0],["XQ",7],["IQ",0],["M1",4],["HE",1],["M1",5],["WR",1,0],["M1",6],["SQ",4],["M1",7],["M1",8],["SQ",5],["M1",9],["M1",10],["HQ"],["SQ",6],["M1",11],["WR",1,1],["M2",0,0],["SQ",7],["TA",1],["SQ",8],["WR",2,0],["SQ",9],["TA",2],["SQ",10],["WR",2,1],["SQ",11],["RT",1],["TA",3],["WQ",1,0],["RT",2],["WQ",1,1],["RT",3],["WQ",2,0],["M2",1,0],["WQ",2,1],["IQ",1],["M2",2,0],["IQ",2],["IQ",3],["BA",0,0],["M2",0,1],["WR",3,0],["SI",0,0],["M2",0,2],["BA",0,1],["M2",0,3],["ST",0,0],["BA",0,2],["SI",0,1],["M2",1,1],["BA",0,3],["SI",0,2],["ST",0,1],["M2",1,2],["BA",1,0],["SI",0,3],["ST",0,2],["M2",1,3],["BA",1,1],["SI",1,0],["WR",3,1],["ST",0,3],["M2",2,1],["BA",1,2],["SI",1,1],["M2",2,2],["ST",1,0],["BA",1,3],["SI",1,2],["M2",2,3],["ST",1,1],["BA",2,0],["SI",1,3],["ST",1,2],["SI",2,0],["ST",1,3],["WQ",3,0],["ST",2,0],["BA",2,1],["BA",2,2],["SI",2,1],["WQ",3,1],["SI",2,2],["ST",2,1],["BA",2,3],["M2",3,0],["ST",2,2],["M2",3,1],["SI",2,3],["BA",3,0],["M2",3,2],["BA",3,1],["ST",2,3],["SI",3,0],["M2",3,3],["BA",3,2],["SI",3,1],["ST",3,0],["BA",3,3],["SI",3,2],["ST",3,1],["SI",3,3],["ST",3,2],["ST",3,3]]
 
 
 def tile_equivariantfeedforward_pa_kernel(tc, h, x1, pre1, w1_0, b1_0, out):
@@ -50,10 +49,6 @@ def tile_equivariantfeedforward_pa_kernel(tc, h, x1, pre1, w1_0, b1_0, out):
         x_raw = [keep.tile([P, 4, P, M1], BF16, name="x_raw%d" % i) for i in range(NT)]
         h_raw = keep.tile([P, NT, D], BF16, name="h_raw")
         bias = keep.tile([P, F], BF16, name="bias")
-        b_row = keep.tile([P, F], BF16, name="b_row")
-        nc.vector.memset(b_row[:].bitcast(mybir.dt.int32), 0)
-        ones = keep.tile([P, P], BF16, name="ones")
-        nc.vector.memset(ones[:], 1.0)
         w_raw = {}
         w_g = {}
         for n in range(NF):
@@ -88,7 +83,7 @@ def tile_equivariantfeedforward_pa_kernel(tc, h, x1, pre1, w1_0, b1_0, out):
             elif what == "h":
                 nc.sync.dma_start(out=h_raw[:], in_=h.rearrange("b n d -> n b d"))
             elif what == "bias":
-                nc.sync.dma_start(out=b_row[0:1, :], in_=b1_0.unsqueeze(0))
+                nc.sync.dma_start(out=bias[:], in_=b1_0.partition_broadcast(P))
             elif what == "x":
                 i = task[2]
                 nc.sync.dma_start(
@@ -235,21 +230,6 @@ def tile_equivariantfeedforward_pa_kernel(tc, h, x1, pre1, w1_0, b1_0, out):
                 out=out_flat[P * i : P * (i + 1), n * FC : (n + 1) * FC], in_=live[("o", n, i)][:]
             )
 
-        def bb(c):
-            t = psum.tile([P, 2 * FC], BF16, name="bb%d" % c, tag="bank")
-            live[("bb", c)] = t
-            for n in range(2):
-                nc.tensor.matmul(
-                    out=t[:, n * FC : (n + 1) * FC],
-                    lhsT=ones[:],
-                    rhs=b_row[:, (2 * c + n) * FC : (2 * c + n + 1) * FC],
-                    start=True,
-                    stop=True,
-                )
-
-        def be(c):
-            leave_psum(BE[c], bias[:, 2 * c * FC : 2 * (c + 1) * FC], live[("bb", c)][:])
-
         def run(task):
             k = task[0]
             a = task[1:]
@@ -285,10 +265,6 @@ def tile_equivariantfeedforward_pa_kernel(tc, h, x1, pre1, w1_0, b1_0, out):
                 regroup(WE[a[0]][a[1]], w_g[(a[0], a[1])][:], w_raw[(a[0], a[1])][:])
             elif k == "WQ":
                 quant(w_c[a[0]][:, a[1], :], w_s[a[0]][:, a[1], :], w_g[(a[0], a[1])][:])
-            elif k == "BB":
-                bb(a[0])
-            elif k == "BE":
-                be(a[0])
             elif k == "M2":
                 m2(a[0], a[1])
             elif k == "BA":

@@ -12,271 +12,269 @@ ACT = mybir.ActivationFunctionType
 ALU = mybir.AluOpType
 
 P = 128
-NT = 4
+PACK = 4
+TOKEN_TILES = 4
+GROUPS = 4
 D = 512
+COMPONENTS = 3
+X_UNITS = TOKEN_TILES * COMPONENTS
 F = 2048
-M1 = 3
-FC = 512
-NF = F // FC
-NU = NT * M1
-FLOPS = 2 * (NT * P * M1) * D * D + 2 * (NT * P) * (2 * D) * F
-
-XE = ["S","S","S","S","S","S","S","S","S","S","S","S"]
-HE = ["S","S"]
-WE = [["V","V"],["V","V"],["V","V"],["G","G"]]
-PRE_ENG = "V"
-MANUAL = True
-ORDER = [["D","x",0],["D","pre"],["D","x",1],["D","w",0,0],["D","x",3],["D","w",0,1],["D","x",2],["D","h"],["D","w",1,0],["D","w",1,1],["D","w",2,0],["D","w",2,1],["D","bias"],["D","w",3,0],["D","w",3,1],["XT",0],["XT",2],["XE",0],["XT",1],["XQ",0],["XE",2],["Pre"],["XE",1],["XT",3],["XQ",1],["Pq"],["XT",4],["XE",3],["XQ",2],["XT",5],["XE",4],["XQ",3],["WR",0,0],["XE",5],["M1",0],["M1",1],["SQ",0],["M1",2],["M1",3],["SQ",1],["XQ",4],["XT",9],["XQ",5],["WQ",0,0],["SQ",2],["XT",10],["XE",9],["XT",11],["WR",0,1],["XE",10],["TA",0],["XE",11],["SQ",3],["XQ",9],["XT",6],["RT",0],["XQ",10],["XQ",11],["XT",8],["WQ",0,1],["XE",6],["XT",7],["XE",8],["XQ",6],["HT",0],["XE",7],["XQ",8],["HT",1],["HE",0],["XQ",7],["IQ",0],["M1",4],["HE",1],["M1",5],["WR",1,0],["M1",6],["SQ",4],["M1",7],["M1",8],["SQ",5],["M1",9],["M1",10],["HQ"],["SQ",6],["M1",11],["WR",1,1],["M2",0,0],["SQ",7],["TA",1],["SQ",8],["WR",2,0],["SQ",9],["TA",2],["SQ",10],["WR",2,1],["SQ",11],["RT",1],["TA",3],["WQ",1,0],["RT",2],["WQ",1,1],["RT",3],["WQ",2,0],["M2",1,0],["WQ",2,1],["IQ",1],["M2",2,0],["IQ",2],["IQ",3],["BA",0,0],["M2",0,1],["WR",3,0],["SI",0,0],["M2",0,2],["BA",0,1],["M2",0,3],["ST",0,0],["BA",0,2],["SI",0,1],["M2",1,1],["BA",0,3],["SI",0,2],["ST",0,1],["M2",1,2],["BA",1,0],["SI",0,3],["ST",0,2],["M2",1,3],["BA",1,1],["SI",1,0],["WR",3,1],["ST",0,3],["M2",2,1],["BA",1,2],["SI",1,1],["M2",2,2],["ST",1,0],["BA",1,3],["SI",1,2],["M2",2,3],["ST",1,1],["BA",2,0],["SI",1,3],["ST",1,2],["SI",2,0],["ST",1,3],["WQ",3,0],["ST",2,0],["BA",2,1],["BA",2,2],["SI",2,1],["WQ",3,1],["SI",2,2],["ST",2,1],["BA",2,3],["M2",3,0],["ST",2,2],["M2",3,1],["SI",2,3],["BA",3,0],["M2",3,2],["BA",3,1],["ST",2,3],["SI",3,0],["M2",3,3],["BA",3,2],["SI",3,1],["ST",3,0],["BA",3,3],["SI",3,2],["ST",3,1],["SI",3,3],["ST",3,2],["ST",3,3]]
+CHUNK = 512
+CHUNKS = F // CHUNK
+PASSES = 2
+VECTOR_UNITS = [(n, g) for n in range(CHUNKS - 1) for g in range(PASSES)]
+GPSIMD_UNITS = [(CHUNKS - 1, g) for g in range(PASSES)]
+PSUM_BANKS = 8
+OUT_BUFFERS = 8
+FLOPS = 2 * (TOKEN_TILES * P * COMPONENTS) * D * D + 2 * (TOKEN_TILES * P) * (PASSES * D) * F
 
 
 def tile_equivariantfeedforward_pa_kernel(tc, h, x1, pre1, w1_0, b1_0, out):
     nc = tc.nc
     with ExitStack() as ctx:
         keep = ctx.enter_context(tc.tile_pool(name="keep", bufs=1))
-        outs = ctx.enter_context(tc.tile_pool(name="outs", bufs=8))
-        psum = ctx.enter_context(tc.psum_pool(name="psum", bufs=8))
+        outs = ctx.enter_context(tc.tile_pool(name="outs", bufs=OUT_BUFFERS))
+        psum = ctx.enter_context(tc.psum_pool(name="psum", bufs=PSUM_BANKS))
 
         ident_bf = keep.tile([P, P], BF16, name="ident_bf")
         masks.make_identity(nc, ident_bf[:])
         ident_f = keep.tile([P, P], F32, name="ident_f")
         masks.make_identity(nc, ident_f[:])
-        warm = keep.tile([P, 1], F32, name="warm")
-        nc.vector.memset(warm[:], 1.0)
-        warm2 = keep.tile([P, 1], F32, name="warm2")
-        nc.scalar.activation(out=warm2[:], in_=warm[:], func=ACT.Sqrt)
+        one = keep.tile([P, 1], F32, name="one")
+        nc.vector.memset(one[:], 1.0)
+        root = keep.tile([P, 1], F32, name="root")
+        nc.scalar.activation(out=root[:], in_=one[:], func=ACT.Sqrt)
 
-        pre_raw = keep.tile([P, 4, D], BF16, name="pre_raw")
-        x_raw = [keep.tile([P, 4, P, M1], BF16, name="x_raw%d" % i) for i in range(NT)]
-        h_raw = keep.tile([P, NT, D], BF16, name="h_raw")
+        pre_raw = keep.tile([P, PACK, D], BF16, name="pre_raw")
+        x_raw = [keep.tile([P, GROUPS, P, COMPONENTS], BF16, name="x_raw%d" % i) for i in range(TOKEN_TILES)]
+        h_raw = keep.tile([P, TOKEN_TILES, D], BF16, name="h_raw")
         bias = keep.tile([P, F], BF16, name="bias")
         w_raw = {}
-        w_g = {}
-        for n in range(NF):
-            for g in range(2):
-                w_raw[(n, g)] = keep.tile([P, 4, FC], BF16, name="w_raw%d_%d" % (g, n))
-                w_g[(n, g)] = keep.tile([P, 4 * FC], BF16, name="w_g%d_%d" % (g, n), align_bytes=64)
-        w_c = [keep.tile([P, 2, FC], U32, name="w_c%d" % n, align_bytes=64) for n in range(NF)]
-        w_s = [keep.tile([P, 2, FC], U8, name="w_s%d" % n, align_bytes=64) for n in range(NF)]
-        pre_g = keep.tile([P, 4 * D], BF16, name="pre_g", align_bytes=64)
-        pre_c = keep.tile([P, D], U32, name="pre_c", align_bytes=64)
-        pre_s = keep.tile([P, D], U8, name="pre_s", align_bytes=64)
-        x_g = keep.tile([P, NU * P * 4], BF16, name="x_g", align_bytes=64)
-        x_c = keep.tile([P, NU * P], U32, name="x_c", align_bytes=64)
-        x_s = keep.tile([P, NU * P], U8, name="x_s", align_bytes=64)
-        inv_g = keep.tile([P, NT * P * 4], BF16, name="inv_g", align_bytes=64)
-        inv_c = keep.tile([P, NT * P], U32, name="inv_c", align_bytes=64)
-        inv_s = keep.tile([P, NT * P], U8, name="inv_s", align_bytes=64)
-        h_g = keep.tile([P, NT * P * 4], BF16, name="h_g", align_bytes=64)
-        h_c = keep.tile([P, NT * P], U32, name="h_c", align_bytes=64)
-        h_s = keep.tile([P, NT * P], U8, name="h_s", align_bytes=64)
-        sq = [keep.tile([P, D], F32, name="sq%d" % v) for v in range(NU)]
-        a_c = [h_c, inv_c]
-        a_s = [h_s, inv_s]
-        out_flat = out.rearrange("b n f -> (b n) f")
-        x_rows = x1.rearrange("b n (j q) m -> (b n j) q m", j=4)
-        live = {}
+        w_grouped = {}
+        for n in range(CHUNKS):
+            for g in range(PASSES):
+                w_raw[(n, g)] = keep.tile([P, PACK, CHUNK], BF16, name="w_raw%d_%d" % (g, n))
+                w_grouped[(n, g)] = keep.tile([P, PACK * CHUNK], BF16, name="w_g%d_%d" % (g, n), align_bytes=64)
+        w_codes = [keep.tile([P, PASSES, CHUNK], U32, name="w_c%d" % n, align_bytes=64) for n in range(CHUNKS)]
+        w_scales = [keep.tile([P, PASSES, CHUNK], U8, name="w_s%d" % n, align_bytes=64) for n in range(CHUNKS)]
+        pre_grouped = keep.tile([P, PACK * D], BF16, name="pre_g", align_bytes=64)
+        pre_codes = keep.tile([P, D], U32, name="pre_c", align_bytes=64)
+        pre_scales = keep.tile([P, D], U8, name="pre_s", align_bytes=64)
+        x_grouped = keep.tile([P, X_UNITS * P * PACK], BF16, name="x_g", align_bytes=64)
+        x_codes = keep.tile([P, X_UNITS * P], U32, name="x_c", align_bytes=64)
+        x_scales = keep.tile([P, X_UNITS * P], U8, name="x_s", align_bytes=64)
+        inv_grouped = keep.tile([P, TOKEN_TILES * P * PACK], BF16, name="inv_g", align_bytes=64)
+        inv_codes = keep.tile([P, TOKEN_TILES * P], U32, name="inv_c", align_bytes=64)
+        inv_scales = keep.tile([P, TOKEN_TILES * P], U8, name="inv_s", align_bytes=64)
+        h_grouped = keep.tile([P, TOKEN_TILES * P * PACK], BF16, name="h_g", align_bytes=64)
+        h_codes = keep.tile([P, TOKEN_TILES * P], U32, name="h_c", align_bytes=64)
+        h_scales = keep.tile([P, TOKEN_TILES * P], U8, name="h_s", align_bytes=64)
+        squares = [keep.tile([P, D], F32, name="sq%d" % v) for v in range(X_UNITS)]
+        act_codes = [h_codes, inv_codes]
+        act_scales = [h_scales, inv_scales]
+        out_rows = out.rearrange("b n f -> (b n) f")
+        x_rows = x1.rearrange("b n (j q) m -> (b n j) q m", j=PACK)
+        banks = {}
 
-        def load(task):
-            what = task[1]
-            if what == "pre":
-                nc.sync.dma_start(out=pre_raw[:], in_=pre1.rearrange("(j p) e -> p j e", p=P))
-            elif what == "h":
-                nc.sync.dma_start(out=h_raw[:], in_=h.rearrange("b n d -> n b d"))
-            elif what == "bias":
-                nc.sync.dma_start(out=bias[:], in_=b1_0.partition_broadcast(P))
-            elif what == "x":
-                i = task[2]
-                nc.sync.dma_start(
-                    out=x_raw[i][:].rearrange("r a q m -> r a (q m)"),
-                    in_=x_rows[512 * i : 512 * (i + 1), :, :].rearrange("(a r) q m -> r a (q m)", r=P),
-                )
-            else:
-                n, g = task[2], task[3]
-                cols = slice(n * FC, (n + 1) * FC)
-                if g == 0:
-                    for u in range(2):
-                        nc.sync.dma_start(
-                            out=w_raw[(n, 0)][:, 2 * u : 2 * u + 2, :],
-                            in_=w1_0[256 * u : 256 * u + 256, cols].rearrange("(q e) c -> q e c", e=2),
-                        )
-                else:
-                    nc.sync.dma_start(
-                        out=w_raw[(n, 1)][:], in_=w1_0[D : 2 * D, cols].rearrange("(j p) c -> p j c", p=P)
-                    )
+        def load_x_group(i, a):
+            first = (GROUPS * i + a) * P
+            nc.sync.dma_start(out=x_raw[i][:, a, :, :], in_=x_rows[first : first + P, :, :])
 
-        def regroup(eng, dst, src):
-            d = dst.rearrange("p (c i t) -> p c t i", i=4, t=4)
-            s = src.rearrange("p t (c i) -> p c t i", i=4)
-            if eng == "V":
-                nc.vector.tensor_copy(out=d, in_=s)
-            elif eng == "S":
-                nc.scalar.copy(out=d, in_=s)
-            else:
-                half = d.shape[1] // 2
-                for q in range(2):
-                    nc.gpsimd.tensor_scalar(
-                        out=d[:, q * half : (q + 1) * half, :, :],
-                        in0=s[:, q * half : (q + 1) * half, :, :],
-                        scalar1=1.0,
-                        scalar2=0.0,
-                        op0=ALU.mult,
-                        op1=ALU.add,
-                    )
-
-        def leave_psum(eng, dst, src):
-            if eng == "V":
-                nc.vector.tensor_copy(out=dst, in_=src)
-            else:
-                nc.scalar.copy(out=dst, in_=src)
-
-        def quant(codes, scales, src):
-            nc.vector.quantize_mx(out=codes.bitcast(FP8X4), scales=scales, in_=src)
-
-        def xt(v):
-            i, m = divmod(v, M1)
-            t = psum.tile([P, 4, P], BF16, name="xt%d" % v, tag="bank")
-            live[("xt", v)] = t
-            for a in range(4):
-                nc.tensor.transpose(t[:, a, :], x_raw[i][:, a, :, m], ident_bf[:])
-
-        def xe(v):
-            leave_psum(XE[v], x_g[:, 512 * v : 512 * (v + 1)], live[("xt", v)][:].rearrange("p a c -> p (a c)"))
-
-        def xq(v):
-            quant(x_c[:, P * v : P * (v + 1)], x_s[:, P * v : P * (v + 1)], x_g[:, 512 * v : 512 * (v + 1)])
-
-        def m1(v):
-            t = psum.tile([P, D], F32, name="p1_%d" % v, tag="bank")
-            live[("p1", v)] = t
-            nc.tensor.matmul_mx(
-                out=t[:],
-                lhsT=x_c[:, P * v : P * (v + 1)].bitcast(FP8X4),
-                lhsT_scale=x_s[:, P * v : P * (v + 1)],
-                rhs=pre_c[:].bitcast(FP8X4),
-                rhs_scale=pre_s[:],
-                start=True,
-                stop=True,
+        def load_x(i):
+            nc.sync.dma_start(
+                out=x_raw[i][:].rearrange("r a q m -> r a (q m)"),
+                in_=x_rows[GROUPS * i * P : GROUPS * (i + 1) * P, :, :].rearrange("(a r) q m -> r a (q m)", r=P),
             )
 
-        def sqr(v):
-            nc.scalar.activation(out=sq[v][:], in_=live[("p1", v)][:], func=ACT.Square)
+        def load_weights(n, g):
+            cols = slice(n * CHUNK, (n + 1) * CHUNK)
+            if g == 0:
+                for u in range(2):
+                    nc.sync.dma_start(
+                        out=w_raw[(n, 0)][:, 2 * u : 2 * u + 2, :],
+                        in_=w1_0[256 * u : 256 * (u + 1), cols].rearrange("(p e) c -> p e c", e=2),
+                    )
+            else:
+                nc.sync.dma_start(out=w_raw[(n, 1)][:], in_=w1_0[D : 2 * D, cols].rearrange("(j p) c -> p j c", p=P))
 
-        def ta(i):
-            t = psum.tile([P, 4, P], F32, name="acc%d" % i, tag="bank")
-            live[("acc", i)] = t
-            for j in range(4):
-                for m in range(M1):
+        def regrouped_views(grouped, raw):
+            return (
+                grouped.rearrange("p (c i t) -> p c t i", i=4, t=PACK),
+                raw.rearrange("p t (c i) -> p c t i", i=4),
+            )
+
+        def quantise(codes, scales, grouped):
+            nc.vector.quantize_mx(out=codes.bitcast(FP8X4), scales=scales, in_=grouped)
+
+        def transpose_x(i):
+            units = [COMPONENTS * i + m for m in range(COMPONENTS)]
+            for v in units:
+                xt = psum.tile([P, GROUPS, P], BF16, name="xt%d" % v, tag="bank")
+                banks[("xt", v)] = xt
+            if i == 0:
+                order = [(a, m) for a in range(GROUPS) for m in range(COMPONENTS)]
+            else:
+                order = [(a, m) for m in range(COMPONENTS) for a in range(GROUPS)]
+            for a, m in order:
+                nc.tensor.transpose(banks[("xt", units[m])][:, a, :], x_raw[i][:, a, :, m], ident_bf[:])
+            for v in units:
+                nc.scalar.copy(
+                    out=x_grouped[:, PACK * P * v : PACK * P * (v + 1)],
+                    in_=banks[("xt", v)][:].rearrange("p a c -> p (a c)"),
+                )
+
+        def quantise_x(i):
+            for v in range(COMPONENTS * i, COMPONENTS * (i + 1)):
+                quantise(
+                    x_codes[:, P * v : P * (v + 1)],
+                    x_scales[:, P * v : P * (v + 1)],
+                    x_grouped[:, PACK * P * v : PACK * P * (v + 1)],
+                )
+
+        def first_matmul(i):
+            for v in range(COMPONENTS * i, COMPONENTS * (i + 1)):
+                pm = psum.tile([P, D], F32, name="pm%d" % v, tag="bank")
+                nc.tensor.matmul_mx(
+                    out=pm[:],
+                    lhsT=x_codes[:, P * v : P * (v + 1)].bitcast(FP8X4),
+                    lhsT_scale=x_scales[:, P * v : P * (v + 1)],
+                    rhs=pre_codes[:].bitcast(FP8X4),
+                    rhs_scale=pre_scales[:],
+                    start=True,
+                    stop=True,
+                )
+                nc.scalar.activation(out=squares[v][:], in_=pm[:], func=ACT.Square)
+
+        def norm(i):
+            total = psum.tile([P, PACK, P], F32, name="total%d" % i, tag="bank")
+            for j in range(PACK):
+                for m in range(COMPONENTS):
                     nc.tensor.matmul(
-                        out=t[:, j, :],
-                        lhsT=sq[M1 * i + m][:, P * j : P * (j + 1)],
+                        out=total[:, j, :],
+                        lhsT=squares[COMPONENTS * i + m][:, P * j : P * (j + 1)],
                         rhs=ident_f[:],
                         is_transpose=True,
                         start=(m == 0),
-                        stop=(m == M1 - 1),
+                        stop=(m == COMPONENTS - 1),
                     )
-
-        def rt(i):
             nc.scalar.activation(
-                out=inv_g[:, 512 * i : 512 * (i + 1)].rearrange("p (t j) -> p t j", j=4),
-                in_=live[("acc", i)][:].rearrange("p j t -> p t j"),
+                out=inv_grouped[:, PACK * P * i : PACK * P * (i + 1)].rearrange("p (t j) -> p t j", j=PACK),
+                in_=total[:].rearrange("p j t -> p t j"),
                 func=ACT.Sqrt,
             )
 
-        def iq(i):
-            quant(inv_c[:, P * i : P * (i + 1)], inv_s[:, P * i : P * (i + 1)], inv_g[:, 512 * i : 512 * (i + 1)])
-
-        def ht(b):
-            t = psum.tile([P, 2, 2, P], F32, name="ht%d" % b, tag="bank")
-            live[("ht", b)] = t
-            for v in range(2):
-                hw = h_raw[:, 2 * b + v, :].bitcast(F32)
-                for u in range(2):
-                    nc.tensor.transpose(t[:, v, u, :], hw[:, P * u : P * (u + 1)], ident_f[:])
-
-        def he(b):
-            leave_psum(
-                HE[b],
-                h_g[:, 1024 * b : 1024 * (b + 1)].bitcast(F32).rearrange("p (v t u) -> p v t u", v=2, u=2),
-                live[("ht", b)][:].rearrange("p v u t -> p v t u"),
+        def quantise_inv(i):
+            quantise(
+                inv_codes[:, P * i : P * (i + 1)],
+                inv_scales[:, P * i : P * (i + 1)],
+                inv_grouped[:, PACK * P * i : PACK * P * (i + 1)],
             )
 
-        def m2(n, i):
-            t = psum.tile([P, FC], F32, name="p2_%d_%d" % (n, i), tag="bank")
-            live[("p2", n, i)] = t
-            for g in range(2):
-                nc.tensor.matmul_mx(
-                    out=t[:],
-                    lhsT=a_c[g][:, P * i : P * (i + 1)].bitcast(FP8X4),
-                    lhsT_scale=a_s[g][:, P * i : P * (i + 1)],
-                    rhs=w_c[n][:, g, :].bitcast(FP8X4),
-                    rhs_scale=w_s[n][:, g, :],
-                    start=(g == 0),
-                    stop=(g == 1),
+        def transpose_h():
+            for b in range(TOKEN_TILES // 2):
+                ht = psum.tile([P, 2, 2, P], F32, name="ht%d" % b, tag="bank")
+                for v in range(2):
+                    words = h_raw[:, 2 * b + v, :].bitcast(F32)
+                    for u in range(2):
+                        nc.tensor.transpose(ht[:, v, u, :], words[:, P * u : P * (u + 1)], ident_f[:])
+                nc.scalar.copy(
+                    out=h_grouped[:, 2 * PACK * P * b : 2 * PACK * P * (b + 1)]
+                    .bitcast(F32)
+                    .rearrange("p (v t u) -> p v t u", v=2, u=2),
+                    in_=ht[:].rearrange("p v u t -> p v t u"),
                 )
 
-        def ba(n, i):
-            o = outs.tile([P, FC], F32, name="o")
-            live[("o", n, i)] = o
-            nc.vector.tensor_tensor(
-                out=o[:], in0=live[("p2", n, i)][:], in1=bias[:, n * FC : (n + 1) * FC], op=ALU.add
-            )
+        def quantise_weights(unit):
+            n, g = unit
+            quantise(w_codes[n][:, g, :], w_scales[n][:, g, :], w_grouped[unit][:])
 
-        def si(n, i):
-            o = live[("o", n, i)]
+        def weight_step(k):
+            if k < len(VECTOR_UNITS):
+                unit = VECTOR_UNITS[k]
+                dst, src = regrouped_views(w_grouped[unit][:], w_raw[unit][:])
+                nc.vector.tensor_copy(out=dst, in_=src)
+            if k >= 1:
+                quantise_weights(VECTOR_UNITS[k - 1])
+
+        def regroup_on_gpsimd(unit):
+            dst, src = regrouped_views(w_grouped[unit][:], w_raw[unit][:])
+            half = dst.shape[1] // 2
+            for q in range(2):
+                nc.gpsimd.tensor_scalar(
+                    out=dst[:, q * half : (q + 1) * half, :, :],
+                    in0=src[:, q * half : (q + 1) * half, :, :],
+                    scalar1=1.0,
+                    scalar2=0.0,
+                    op0=ALU.mult,
+                    op1=ALU.add,
+                )
+
+        def second_matmul(n, i):
+            acc = psum.tile([P, CHUNK], F32, name="acc%d_%d" % (n, i), tag="bank")
+            for g in range(PASSES):
+                nc.tensor.matmul_mx(
+                    out=acc[:],
+                    lhsT=act_codes[g][:, P * i : P * (i + 1)].bitcast(FP8X4),
+                    lhsT_scale=act_scales[g][:, P * i : P * (i + 1)],
+                    rhs=w_codes[n][:, g, :].bitcast(FP8X4),
+                    rhs_scale=w_scales[n][:, g, :],
+                    start=(g == 0),
+                    stop=(g == PASSES - 1),
+                )
+            o = outs.tile([P, CHUNK], F32, name="o")
+            nc.vector.tensor_tensor(out=o[:], in0=acc[:], in1=bias[:, n * CHUNK : (n + 1) * CHUNK], op=ALU.add)
             nc.scalar.activation(out=o[:], in_=o[:], func=ACT.Silu)
+            nc.sync.dma_start(out=out_rows[P * i : P * (i + 1), n * CHUNK : (n + 1) * CHUNK], in_=o[:])
 
-        def st(n, i):
-            nc.sync.dma_start(
-                out=out_flat[P * i : P * (i + 1), n * FC : (n + 1) * FC], in_=live[("o", n, i)][:]
-            )
+        ctx.enter_context(tc.manual_schedule())
 
-        def run(task):
-            k = task[0]
-            a = task[1:]
-            if k == "D":
-                load(task)
-            elif k == "Pre":
-                regroup(PRE_ENG, pre_g[:], pre_raw[:])
-            elif k == "Pq":
-                quant(pre_c[:], pre_s[:], pre_g[:])
-            elif k == "XT":
-                xt(a[0])
-            elif k == "XE":
-                xe(a[0])
-            elif k == "XQ":
-                xq(a[0])
-            elif k == "M1":
-                m1(a[0])
-            elif k == "SQ":
-                sqr(a[0])
-            elif k == "TA":
-                ta(a[0])
-            elif k == "RT":
-                rt(a[0])
-            elif k == "IQ":
-                iq(a[0])
-            elif k == "HT":
-                ht(a[0])
-            elif k == "HE":
-                he(a[0])
-            elif k == "HQ":
-                quant(h_c[:], h_s[:], h_g[:])
-            elif k == "WR":
-                regroup(WE[a[0]][a[1]], w_g[(a[0], a[1])][:], w_raw[(a[0], a[1])][:])
-            elif k == "WQ":
-                quant(w_c[a[0]][:, a[1], :], w_s[a[0]][:, a[1], :], w_g[(a[0], a[1])][:])
-            elif k == "M2":
-                m2(a[0], a[1])
-            elif k == "BA":
-                ba(a[0], a[1])
-            elif k == "SI":
-                si(a[0], a[1])
-            elif k == "ST":
-                st(a[0], a[1])
-            else:
-                raise ValueError(k)
+        for a in range(GROUPS):
+            load_x_group(0, a)
+        nc.sync.dma_start(out=pre_raw[:], in_=pre1.rearrange("(j p) e -> p j e", p=P))
+        load_x(1)
+        load_weights(0, 0)
+        load_x(2)
+        load_weights(0, 1)
+        load_x(3)
+        nc.sync.dma_start(out=h_raw[:], in_=h.rearrange("b n d -> n b d"))
+        for unit in VECTOR_UNITS[2:]:
+            load_weights(unit[0], unit[1])
+        nc.sync.dma_start(out=bias[:], in_=b1_0.partition_broadcast(P))
+        for unit in GPSIMD_UNITS:
+            load_weights(unit[0], unit[1])
 
-        if MANUAL:
-            ctx.enter_context(tc.manual_schedule())
-        for task in ORDER:
-            run(task)
+        transpose_x(0)
+        dst, src = regrouped_views(pre_grouped[:], pre_raw[:])
+        nc.vector.tensor_copy(out=dst, in_=src)
+        quantise_x(0)
+        quantise(pre_codes[:], pre_scales[:], pre_grouped[:])
+        transpose_x(1)
+        quantise_x(1)
+        first_matmul(0)
+        weight_step(0)
+        transpose_x(2)
+        quantise_x(2)
+        weight_step(1)
+        norm(0)
+        transpose_x(3)
+        quantise_x(3)
+        weight_step(2)
+        quantise_inv(0)
+        transpose_h()
+        quantise(h_codes[:], h_scales[:], h_grouped[:])
+        for i in range(1, TOKEN_TILES):
+            first_matmul(i)
+        for k in range(3, len(VECTOR_UNITS) + 1):
+            weight_step(k)
+        for i in range(1, TOKEN_TILES):
+            norm(i)
+        for i in range(1, TOKEN_TILES):
+            quantise_inv(i)
+        for unit in GPSIMD_UNITS:
+            regroup_on_gpsimd(unit)
+
+        for n in range(CHUNKS):
+            for i in range(TOKEN_TILES):
+                second_matmul(n, i)
+                if n == CHUNKS - 2 and i % 2 == 0:
+                    quantise_weights(GPSIMD_UNITS[i // 2])

@@ -22,10 +22,11 @@ F = 2048
 CHUNK = 512
 CHUNKS = F // CHUNK
 PASSES = 2
-VECTOR_UNITS = [(n, g) for n in range(CHUNKS - 1) for g in range(PASSES)]
-GPSIMD_UNITS = [(CHUNKS - 1, g) for g in range(PASSES)]
+VECTOR_UNITS = [(n, g) for n in range(2) for g in range(PASSES)]
+TENSOR_UNITS = [(2, g) for g in range(PASSES)]
+GPSIMD_UNITS = [(3, g) for g in range(PASSES)]
 PSUM_BANKS = 8
-OUT_BUFFERS = 8
+OUT_BUFFERS = 16
 FLOPS = 2 * (TOKEN_TILES * P * COMPONENTS) * D * D + 2 * (TOKEN_TILES * P) * (PASSES * D) * F
 
 
@@ -107,18 +108,16 @@ def tile_equivariantfeedforward_pa_kernel(tc, h, x1, pre1, w1_0, b1_0, out):
             nc.vector.quantize_mx(out=codes.bitcast(FP8X4), scales=scales, in_=grouped)
 
         def transpose_x(i):
-            units = [COMPONENTS * i + m for m in range(COMPONENTS)]
-            for v in units:
+            for m in range(COMPONENTS):
+                v = COMPONENTS * i + m
                 xt = psum.tile([P, GROUPS, P], BF16, name="xt%d" % v, tag="bank")
                 banks[("xt", v)] = xt
-            if i == 0:
-                order = [(a, m) for a in range(GROUPS) for m in range(COMPONENTS)]
-            else:
-                order = [(a, m) for m in range(COMPONENTS) for a in range(GROUPS)]
-            for a, m in order:
-                nc.tensor.transpose(banks[("xt", units[m])][:, a, :], x_raw[i][:, a, :, m], ident_bf[:])
-            for v in units:
-                nc.scalar.copy(
+                for a in range(GROUPS):
+                    nc.tensor.transpose(xt[:, a, :], x_raw[i][:, a, :, m], ident_bf[:])
+
+        def copy_x(i, copy):
+            for v in range(COMPONENTS * i, COMPONENTS * (i + 1)):
+                copy(
                     out=x_grouped[:, PACK * P * v : PACK * P * (v + 1)],
                     in_=banks[("xt", v)][:].rearrange("p a c -> p (a c)"),
                 )
@@ -134,6 +133,7 @@ def tile_equivariantfeedforward_pa_kernel(tc, h, x1, pre1, w1_0, b1_0, out):
         def first_matmul(i):
             for v in range(COMPONENTS * i, COMPONENTS * (i + 1)):
                 pm = psum.tile([P, D], F32, name="pm%d" % v, tag="bank")
+                banks[("pm", v)] = pm
                 nc.tensor.matmul_mx(
                     out=pm[:],
                     lhsT=x_codes[:, P * v : P * (v + 1)].bitcast(FP8X4),
@@ -143,10 +143,14 @@ def tile_equivariantfeedforward_pa_kernel(tc, h, x1, pre1, w1_0, b1_0, out):
                     start=True,
                     stop=True,
                 )
-                nc.scalar.activation(out=squares[v][:], in_=pm[:], func=ACT.Square)
+
+        def square(i):
+            for v in range(COMPONENTS * i, COMPONENTS * (i + 1)):
+                nc.scalar.activation(out=squares[v][:], in_=banks[("pm", v)][:], func=ACT.Square)
 
         def norm(i):
             total = psum.tile([P, PACK, P], F32, name="total%d" % i, tag="bank")
+            banks[("total", i)] = total
             for j in range(PACK):
                 for m in range(COMPONENTS):
                     nc.tensor.matmul(
@@ -157,9 +161,11 @@ def tile_equivariantfeedforward_pa_kernel(tc, h, x1, pre1, w1_0, b1_0, out):
                         start=(m == 0),
                         stop=(m == COMPONENTS - 1),
                     )
+
+        def root_of_norm(i):
             nc.scalar.activation(
                 out=inv_grouped[:, PACK * P * i : PACK * P * (i + 1)].rearrange("p (t j) -> p t j", j=PACK),
-                in_=total[:].rearrange("p j t -> p t j"),
+                in_=banks[("total", i)][:].rearrange("p j t -> p t j"),
                 func=ACT.Sqrt,
             )
 
@@ -173,28 +179,49 @@ def tile_equivariantfeedforward_pa_kernel(tc, h, x1, pre1, w1_0, b1_0, out):
         def transpose_h():
             for b in range(TOKEN_TILES // 2):
                 ht = psum.tile([P, 2, 2, P], F32, name="ht%d" % b, tag="bank")
+                banks[("ht", b)] = ht
                 for v in range(2):
                     words = h_raw[:, 2 * b + v, :].bitcast(F32)
                     for u in range(2):
                         nc.tensor.transpose(ht[:, v, u, :], words[:, P * u : P * (u + 1)], ident_f[:])
+
+        def copy_h():
+            for b in range(TOKEN_TILES // 2):
                 nc.scalar.copy(
                     out=h_grouped[:, 2 * PACK * P * b : 2 * PACK * P * (b + 1)]
                     .bitcast(F32)
                     .rearrange("p (v t u) -> p v t u", v=2, u=2),
-                    in_=ht[:].rearrange("p v u t -> p v t u"),
+                    in_=banks[("ht", b)][:].rearrange("p v u t -> p v t u"),
                 )
 
         def quantise_weights(unit):
             n, g = unit
             quantise(w_codes[n][:, g, :], w_scales[n][:, g, :], w_grouped[unit][:])
 
-        def weight_step(k):
-            if k < len(VECTOR_UNITS):
-                unit = VECTOR_UNITS[k]
-                dst, src = regrouped_views(w_grouped[unit][:], w_raw[unit][:])
-                nc.vector.tensor_copy(out=dst, in_=src)
-            if k >= 1:
-                quantise_weights(VECTOR_UNITS[k - 1])
+        def regroup(unit):
+            dst, src = regrouped_views(w_grouped[unit][:], w_raw[unit][:])
+            nc.vector.tensor_copy(out=dst, in_=src)
+
+        def regroup_on_tensor(unit):
+            for q in range(2):
+                wt = psum.tile([P, CHUNK // 2, PACK], BF16, name="wt%d%d_%d" % (unit[0], unit[1], q), tag="bank")
+                banks[("wt", unit, q)] = wt
+                for s in range(2):
+                    cols = slice(256 * q + 128 * s, 256 * q + 128 * (s + 1))
+                    nc.tensor.matmul(
+                        out=wt[:, 128 * s : 128 * (s + 1), :].rearrange("p c t -> p (c t)"),
+                        lhsT=ident_bf[:],
+                        rhs=w_raw[unit][:, :, cols].rearrange("p t c -> p c t"),
+                        start=True,
+                        stop=True,
+                    )
+
+        def copy_regrouped(unit):
+            for q in range(2):
+                nc.scalar.copy(
+                    out=w_grouped[unit][:, 1024 * q : 1024 * (q + 1)],
+                    in_=banks[("wt", unit, q)][:].rearrange("p c t -> p (c t)"),
+                )
 
         def regroup_on_gpsimd(unit):
             dst, src = regrouped_views(w_grouped[unit][:], w_raw[unit][:])
@@ -211,6 +238,7 @@ def tile_equivariantfeedforward_pa_kernel(tc, h, x1, pre1, w1_0, b1_0, out):
 
         def second_matmul(n, i):
             acc = psum.tile([P, CHUNK], F32, name="acc%d_%d" % (n, i), tag="bank")
+            banks[("acc", n, i)] = acc
             for g in range(PASSES):
                 nc.tensor.matmul_mx(
                     out=acc[:],
@@ -221,60 +249,104 @@ def tile_equivariantfeedforward_pa_kernel(tc, h, x1, pre1, w1_0, b1_0, out):
                     start=(g == 0),
                     stop=(g == PASSES - 1),
                 )
+
+        def add_bias(n, i):
             o = outs.tile([P, CHUNK], F32, name="o")
-            nc.vector.tensor_tensor(out=o[:], in0=acc[:], in1=bias[:, n * CHUNK : (n + 1) * CHUNK], op=ALU.add)
+            banks[("o", n, i)] = o
+            nc.vector.tensor_tensor(
+                out=o[:], in0=banks[("acc", n, i)][:], in1=bias[:, n * CHUNK : (n + 1) * CHUNK], op=ALU.add
+            )
+
+        def silu_and_store(n, i):
+            o = banks[("o", n, i)]
             nc.scalar.activation(out=o[:], in_=o[:], func=ACT.Silu)
             nc.sync.dma_start(out=out_rows[P * i : P * (i + 1), n * CHUNK : (n + 1) * CHUNK], in_=o[:])
 
         ctx.enter_context(tc.manual_schedule())
 
-        for a in range(GROUPS):
-            load_x_group(0, a)
         nc.sync.dma_start(out=pre_raw[:], in_=pre1.rearrange("(j p) e -> p j e", p=P))
+        load_x(0)
         load_x(1)
         load_weights(0, 0)
         load_x(2)
         load_weights(0, 1)
         load_x(3)
+        load_weights(1, 0)
         nc.sync.dma_start(out=h_raw[:], in_=h.rearrange("b n d -> n b d"))
-        for unit in VECTOR_UNITS[2:]:
+        load_weights(1, 1)
+        for unit in TENSOR_UNITS:
             load_weights(unit[0], unit[1])
         nc.sync.dma_start(out=bias[:], in_=b1_0.partition_broadcast(P))
         for unit in GPSIMD_UNITS:
             load_weights(unit[0], unit[1])
 
-        transpose_x(0)
         dst, src = regrouped_views(pre_grouped[:], pre_raw[:])
         nc.vector.tensor_copy(out=dst, in_=src)
-        quantise_x(0)
         quantise(pre_codes[:], pre_scales[:], pre_grouped[:])
+        transpose_x(0)
+        copy_x(0, nc.scalar.copy)
+        quantise_x(0)
         transpose_x(1)
-        quantise_x(1)
         first_matmul(0)
-        weight_step(0)
+        copy_x(1, nc.scalar.copy)
+        quantise_x(1)
+        square(0)
+        first_matmul(1)
+        regroup((0, 0))
+        square(1)
         transpose_x(2)
+        copy_x(2, nc.vector.tensor_copy)
         quantise_x(2)
-        weight_step(1)
+        quantise_weights((0, 0))
         norm(0)
+        root_of_norm(0)
+        first_matmul(2)
         transpose_x(3)
-        quantise_x(3)
-        weight_step(2)
+        square(2)
         quantise_inv(0)
+        regroup((0, 1))
+        copy_x(3, nc.scalar.copy)
+        quantise_x(3)
+        quantise_weights((0, 1))
+        norm(1)
+        root_of_norm(1)
+        regroup((1, 0))
+        first_matmul(3)
+        square(3)
+        quantise_inv(1)
+        regroup((1, 1))
+        quantise_weights((1, 0))
+        norm(2)
         transpose_h()
+        root_of_norm(2)
+        copy_h()
+        quantise_inv(2)
+        quantise_weights((1, 1))
         quantise(h_codes[:], h_scales[:], h_grouped[:])
-        for i in range(1, TOKEN_TILES):
-            first_matmul(i)
-        for k in range(3, len(VECTOR_UNITS) + 1):
-            weight_step(k)
-        for i in range(1, TOKEN_TILES):
-            norm(i)
-        for i in range(1, TOKEN_TILES):
-            quantise_inv(i)
+        norm(3)
+        root_of_norm(3)
+        for unit in TENSOR_UNITS:
+            regroup_on_tensor(unit)
+            copy_regrouped(unit)
         for unit in GPSIMD_UNITS:
             regroup_on_gpsimd(unit)
-
-        for n in range(CHUNKS):
+        quantise_inv(3)
+        for i in range(TOKEN_TILES):
+            second_matmul(0, i)
+        quantise_weights((2, 0))
+        for i in range(TOKEN_TILES):
+            add_bias(0, i)
+            silu_and_store(0, i)
+        quantise_weights((2, 1))
+        for i in range(TOKEN_TILES):
+            second_matmul(1, i)
+        for i in range(TOKEN_TILES):
+            add_bias(1, i)
+            silu_and_store(1, i)
+        for n in (2, 3):
             for i in range(TOKEN_TILES):
                 second_matmul(n, i)
-                if n == CHUNKS - 2 and i % 2 == 0:
-                    quantise_weights(GPSIMD_UNITS[i // 2])
+                add_bias(n, i)
+                silu_and_store(n, i)
+                if n == 2 and i < 2:
+                    quantise_weights(GPSIMD_UNITS[i])

@@ -23,7 +23,6 @@ CHUNK = 512
 CHUNKS = F // CHUNK
 PASSES = 2
 VECTOR_UNITS = [(n, g) for n in range(2) for g in range(PASSES)]
-TENSOR_UNITS = [(2, g) for g in range(PASSES)]
 GPSIMD_UNITS = [(3, g) for g in range(PASSES)]
 PSUM_BANKS = 8
 OUT_BUFFERS = 16
@@ -202,27 +201,6 @@ def tile_equivariantfeedforward_pa_kernel(tc, h, x1, pre1, w1_0, b1_0, out):
             dst, src = regrouped_views(w_grouped[unit][:], w_raw[unit][:])
             nc.vector.tensor_copy(out=dst, in_=src)
 
-        def regroup_on_tensor(unit):
-            for q in range(2):
-                wt = psum.tile([P, CHUNK // 2, PACK], BF16, name="wt%d%d_%d" % (unit[0], unit[1], q), tag="bank")
-                banks[("wt", unit, q)] = wt
-                for s in range(2):
-                    cols = slice(256 * q + 128 * s, 256 * q + 128 * (s + 1))
-                    nc.tensor.matmul(
-                        out=wt[:, 128 * s : 128 * (s + 1), :].rearrange("p c t -> p (c t)"),
-                        lhsT=ident_bf[:],
-                        rhs=w_raw[unit][:, :, cols].rearrange("p t c -> p c t"),
-                        start=True,
-                        stop=True,
-                    )
-
-        def copy_regrouped(unit):
-            for q in range(2):
-                nc.scalar.copy(
-                    out=w_grouped[unit][:, 1024 * q : 1024 * (q + 1)],
-                    in_=banks[("wt", unit, q)][:].rearrange("p c t -> p (c t)"),
-                )
-
         def regroup_on_gpsimd(unit):
             dst, src = regrouped_views(w_grouped[unit][:], w_raw[unit][:])
             half = dst.shape[1] // 2
@@ -274,8 +252,8 @@ def tile_equivariantfeedforward_pa_kernel(tc, h, x1, pre1, w1_0, b1_0, out):
         load_weights(1, 0)
         nc.sync.dma_start(out=h_raw[:], in_=h.rearrange("b n d -> n b d"))
         load_weights(1, 1)
-        for unit in TENSOR_UNITS:
-            load_weights(unit[0], unit[1])
+        load_weights(2, 0)
+        load_weights(2, 1)
         nc.sync.dma_start(out=bias[:], in_=b1_0.partition_broadcast(P))
         for unit in GPSIMD_UNITS:
             load_weights(unit[0], unit[1])
@@ -325,19 +303,18 @@ def tile_equivariantfeedforward_pa_kernel(tc, h, x1, pre1, w1_0, b1_0, out):
         quantise(h_codes[:], h_scales[:], h_grouped[:])
         norm(3)
         root_of_norm(3)
-        for unit in TENSOR_UNITS:
-            regroup_on_tensor(unit)
-            copy_regrouped(unit)
-        for unit in GPSIMD_UNITS:
-            regroup_on_gpsimd(unit)
+        regroup((2, 0))
         quantise_inv(3)
         for i in range(TOKEN_TILES):
             second_matmul(0, i)
+        regroup((2, 1))
         quantise_weights((2, 0))
+        quantise_weights((2, 1))
+        for unit in GPSIMD_UNITS:
+            regroup_on_gpsimd(unit)
         for i in range(TOKEN_TILES):
             add_bias(0, i)
             silu_and_store(0, i)
-        quantise_weights((2, 1))
         for i in range(TOKEN_TILES):
             second_matmul(1, i)
         for i in range(TOKEN_TILES):

@@ -197,9 +197,9 @@ def tile_equivariantfeedforward_pa_kernel(tc, h, x1, pre1, w1_0, b1_0, out):
             n, g = unit
             quantise(w_codes[n][:, g, :], w_scales[n][:, g, :], w_grouped[unit][:])
 
-        def regroup(unit):
+        def regroup(unit, copy):
             dst, src = regrouped_views(w_grouped[unit][:], w_raw[unit][:])
-            nc.vector.tensor_copy(out=dst, in_=src)
+            copy(out=dst, in_=src)
 
         def regroup_on_gpsimd(unit):
             dst, src = regrouped_views(w_grouped[unit][:], w_raw[unit][:])
@@ -249,11 +249,11 @@ def tile_equivariantfeedforward_pa_kernel(tc, h, x1, pre1, w1_0, b1_0, out):
         load_x(2)
         load_weights(0, 1)
         load_x(3)
-        load_weights(1, 0)
         nc.sync.dma_start(out=h_raw[:], in_=h.rearrange("b n d -> n b d"))
+        load_weights(1, 0)
         load_weights(1, 1)
-        load_weights(2, 0)
         load_weights(2, 1)
+        load_weights(2, 0)
         nc.sync.dma_start(out=bias[:], in_=b1_0.partition_broadcast(P))
         for unit in GPSIMD_UNITS:
             load_weights(unit[0], unit[1])
@@ -270,7 +270,7 @@ def tile_equivariantfeedforward_pa_kernel(tc, h, x1, pre1, w1_0, b1_0, out):
         quantise_x(1)
         square(0)
         first_matmul(1)
-        regroup((0, 0))
+        regroup((0, 0), nc.vector.tensor_copy)
         square(1)
         transpose_x(2)
         copy_x(2, nc.vector.tensor_copy)
@@ -281,19 +281,19 @@ def tile_equivariantfeedforward_pa_kernel(tc, h, x1, pre1, w1_0, b1_0, out):
         first_matmul(2)
         transpose_x(3)
         square(2)
+        regroup((0, 1), nc.vector.tensor_copy)
         quantise_inv(0)
-        regroup((0, 1))
-        copy_x(3, nc.scalar.copy)
+        copy_x(3, nc.vector.tensor_copy)
         quantise_x(3)
         quantise_weights((0, 1))
         norm(1)
         root_of_norm(1)
-        regroup((1, 0))
+        regroup((1, 0), nc.vector.tensor_copy)
         first_matmul(3)
         square(3)
         quantise_inv(1)
-        regroup((1, 1))
         quantise_weights((1, 0))
+        regroup((1, 1), nc.vector.tensor_copy)
         norm(2)
         transpose_h()
         root_of_norm(2)
@@ -303,11 +303,11 @@ def tile_equivariantfeedforward_pa_kernel(tc, h, x1, pre1, w1_0, b1_0, out):
         quantise(h_codes[:], h_scales[:], h_grouped[:])
         norm(3)
         root_of_norm(3)
-        regroup((2, 0))
+        regroup((2, 0), nc.vector.tensor_copy)
         quantise_inv(3)
+        regroup((2, 1), nc.scalar.copy)
         for i in range(TOKEN_TILES):
             second_matmul(0, i)
-        regroup((2, 1))
         quantise_weights((2, 0))
         quantise_weights((2, 1))
         for unit in GPSIMD_UNITS:

@@ -99,8 +99,8 @@ def tile_equivariantfeedforward_pa_kernel(tc, h, x1, pre1, w1_0, b1_0, out):
 
         def regrouped_views(grouped, raw):
             return (
-                grouped.rearrange("p (c i t) -> p c t i", i=4, t=PACK),
-                raw.rearrange("p t (c i) -> p c t i", i=4),
+                grouped.rearrange("p (c i t) -> p c t i", i=8, t=PACK),
+                raw.rearrange("p t (c i) -> p c t i", i=8),
             )
 
         def quantise(codes, scales, grouped):

from contextlib import ExitStack

import concourse.masks as masks
import concourse.mybir as mybir

F32 = mybir.dt.float32
BF16 = mybir.dt.bfloat16
U32 = mybir.dt.uint32
U8 = mybir.dt.uint8
FP8X4 = mybir.dt.float8_e4m3fn_x4
ACT = mybir.ActivationFunctionType
ALU = mybir.AluOpType

P = 128
PACK = 4
TOKEN_TILES = 4
GROUPS = 4
D = 512
COMPONENTS = 3
X_UNITS = TOKEN_TILES * COMPONENTS
F = 2048
CHUNK = 512
CHUNKS = F // CHUNK
PASSES = 2
VECTOR_UNITS = [(n, g) for n in range(2) for g in range(PASSES)]
GPSIMD_UNITS = [(3, g) for g in range(PASSES)]
PSUM_BANKS = 8
OUT_BUFFERS = 16
FLOPS = 2 * (TOKEN_TILES * P * COMPONENTS) * D * D + 2 * (TOKEN_TILES * P) * (PASSES * D) * F


def tile_equivariantfeedforward_pa_kernel(tc, h, x1, pre1, w1_0, b1_0, out):
    nc = tc.nc
    with ExitStack() as ctx:
        keep = ctx.enter_context(tc.tile_pool(name="keep", bufs=1))
        outs = ctx.enter_context(tc.tile_pool(name="outs", bufs=OUT_BUFFERS))
        psum = ctx.enter_context(tc.psum_pool(name="psum", bufs=PSUM_BANKS))

        ident_bf = keep.tile([P, P], BF16, name="ident_bf")
        masks.make_identity(nc, ident_bf[:])
        ident_f = keep.tile([P, P], F32, name="ident_f")
        masks.make_identity(nc, ident_f[:])
        one = keep.tile([P, 1], F32, name="one")
        nc.vector.memset(one[:], 1.0)
        root = keep.tile([P, 1], F32, name="root")
        nc.scalar.activation(out=root[:], in_=one[:], func=ACT.Sqrt)

        pre_raw = keep.tile([P, PACK, D], BF16, name="pre_raw")
        x_raw = [keep.tile([P, GROUPS, P, COMPONENTS], BF16, name="x_raw%d" % i) for i in range(TOKEN_TILES)]
        h_raw = keep.tile([P, TOKEN_TILES, D], BF16, name="h_raw")
        bias = keep.tile([P, F], BF16, name="bias")
        w_raw = {}
        w_grouped = {}
        for n in range(CHUNKS):
            for g in range(PASSES):
                w_raw[(n, g)] = keep.tile([P, PACK, CHUNK], BF16, name="w_raw%d_%d" % (g, n))
                w_grouped[(n, g)] = keep.tile([P, PACK * CHUNK], BF16, name="w_g%d_%d" % (g, n), align_bytes=64)
        w_codes = [keep.tile([P, PASSES, CHUNK], U32, name="w_c%d" % n, align_bytes=64) for n in range(CHUNKS)]
        w_scales = [keep.tile([P, PASSES, CHUNK], U8, name="w_s%d" % n, align_bytes=64) for n in range(CHUNKS)]
        pre_grouped = keep.tile([P, PACK * D], BF16, name="pre_g", align_bytes=64)
        pre_codes = keep.tile([P, D], U32, name="pre_c", align_bytes=64)
        pre_scales = keep.tile([P, D], U8, name="pre_s", align_bytes=64)
        x_grouped = keep.tile([P, X_UNITS * P * PACK], BF16, name="x_g", align_bytes=64)
        x_codes = keep.tile([P, X_UNITS * P], U32, name="x_c", align_bytes=64)
        x_scales = keep.tile([P, X_UNITS * P], U8, name="x_s", align_bytes=64)
        inv_grouped = keep.tile([P, TOKEN_TILES * P * PACK], BF16, name="inv_g", align_bytes=64)
        inv_codes = keep.tile([P, TOKEN_TILES * P], U32, name="inv_c", align_bytes=64)
        inv_scales = keep.tile([P, TOKEN_TILES * P], U8, name="inv_s", align_bytes=64)
        h_grouped = keep.tile([P, TOKEN_TILES * P * PACK], BF16, name="h_g", align_bytes=64)
        h_codes = keep.tile([P, TOKEN_TILES * P], U32, name="h_c", align_bytes=64)
        h_scales = keep.tile([P, TOKEN_TILES * P], U8, name="h_s", align_bytes=64)
        squares = [keep.tile([P, D], F32, name="sq%d" % v) for v in range(X_UNITS)]
        act_codes = [h_codes, inv_codes]
        act_scales = [h_scales, inv_scales]
        out_rows = out.rearrange("b n f -> (b n) f")
        x_rows = x1.rearrange("b n (j q) m -> (b n j) q m", j=PACK)
        banks = {}

        def load_x_group(i, a):
            first = (GROUPS * i + a) * P
            nc.sync.dma_start(out=x_raw[i][:, a, :, :], in_=x_rows[first : first + P, :, :])

        def load_x(i):
            nc.sync.dma_start(
                out=x_raw[i][:].rearrange("r a q m -> r a (q m)"),
                in_=x_rows[GROUPS * i * P : GROUPS * (i + 1) * P, :, :].rearrange("(a r) q m -> r a (q m)", r=P),
            )

        def load_weights(n, g):
            cols = slice(n * CHUNK, (n + 1) * CHUNK)
            if g == 0:
                for u in range(2):
                    nc.sync.dma_start(
                        out=w_raw[(n, 0)][:, 2 * u : 2 * u + 2, :],
                        in_=w1_0[256 * u : 256 * (u + 1), cols].rearrange("(p e) c -> p e c", e=2),
                    )
            else:
                nc.sync.dma_start(out=w_raw[(n, 1)][:], in_=w1_0[D : 2 * D, cols].rearrange("(j p) c -> p j c", p=P))

        def regrouped_views(grouped, raw):
            return (
                grouped.rearrange("p (c i t) -> p c t i", i=8, t=PACK),
                raw.rearrange("p t (c i) -> p c t i", i=8),
            )

        def quantise(codes, scales, grouped):
            nc.vector.quantize_mx(out=codes.bitcast(FP8X4), scales=scales, in_=grouped)

        def transpose_x(i):
            for m in range(COMPONENTS):
                v = COMPONENTS * i + m
                xt = psum.tile([P, GROUPS, P], BF16, name="xt%d" % v, tag="bank")
                banks[("xt", v)] = xt
                for a in range(GROUPS):
                    nc.tensor.transpose(xt[:, a, :], x_raw[i][:, a, :, m], ident_bf[:])

        def copy_x(i, copy):
            for v in range(COMPONENTS * i, COMPONENTS * (i + 1)):
                copy(
                    out=x_grouped[:, PACK * P * v : PACK * P * (v + 1)],
                    in_=banks[("xt", v)][:].rearrange("p a c -> p (a c)"),
                )

        def quantise_x(i):
            for v in range(COMPONENTS * i, COMPONENTS * (i + 1)):
                quantise(
                    x_codes[:, P * v : P * (v + 1)],
                    x_scales[:, P * v : P * (v + 1)],
                    x_grouped[:, PACK * P * v : PACK * P * (v + 1)],
                )

        def first_matmul(i):
            for v in range(COMPONENTS * i, COMPONENTS * (i + 1)):
                pm = psum.tile([P, D], F32, name="pm%d" % v, tag="bank")
                banks[("pm", v)] = pm
                nc.tensor.matmul_mx(
                    out=pm[:],
                    lhsT=x_codes[:, P * v : P * (v + 1)].bitcast(FP8X4),
                    lhsT_scale=x_scales[:, P * v : P * (v + 1)],
                    rhs=pre_codes[:].bitcast(FP8X4),
                    rhs_scale=pre_scales[:],
                    start=True,
                    stop=True,
                )

        def square(i):
            for v in range(COMPONENTS * i, COMPONENTS * (i + 1)):
                nc.scalar.activation(out=squares[v][:], in_=banks[("pm", v)][:], func=ACT.Square)

        def norm(i):
            total = psum.tile([P, PACK, P], F32, name="total%d" % i, tag="bank")
            banks[("total", i)] = total
            for j in range(PACK):
                for m in range(COMPONENTS):
                    nc.tensor.matmul(
                        out=total[:, j, :],
                        lhsT=squares[COMPONENTS * i + m][:, P * j : P * (j + 1)],
                        rhs=ident_f[:],
                        is_transpose=True,
                        start=(m == 0),
                        stop=(m == COMPONENTS - 1),
                    )

        def root_of_norm(i):
            nc.scalar.activation(
                out=inv_grouped[:, PACK * P * i : PACK * P * (i + 1)].rearrange("p (t j) -> p t j", j=PACK),
                in_=banks[("total", i)][:].rearrange("p j t -> p t j"),
                func=ACT.Sqrt,
            )

        def quantise_inv(i):
            quantise(
                inv_codes[:, P * i : P * (i + 1)],
                inv_scales[:, P * i : P * (i + 1)],
                inv_grouped[:, PACK * P * i : PACK * P * (i + 1)],
            )

        def transpose_h():
            for b in range(TOKEN_TILES // 2):
                ht = psum.tile([P, 2, 2, P], F32, name="ht%d" % b, tag="bank")
                banks[("ht", b)] = ht
                for v in range(2):
                    words = h_raw[:, 2 * b + v, :].bitcast(F32)
                    for u in range(2):
                        nc.tensor.transpose(ht[:, v, u, :], words[:, P * u : P * (u + 1)], ident_f[:])

        def copy_h():
            for b in range(TOKEN_TILES // 2):
                nc.scalar.copy(
                    out=h_grouped[:, 2 * PACK * P * b : 2 * PACK * P * (b + 1)]
                    .bitcast(F32)
                    .rearrange("p (v t u) -> p v t u", v=2, u=2),
                    in_=banks[("ht", b)][:].rearrange("p v u t -> p v t u"),
                )

        def quantise_weights(unit):
            n, g = unit
            quantise(w_codes[n][:, g, :], w_scales[n][:, g, :], w_grouped[unit][:])

        def regroup(unit, copy):
            dst, src = regrouped_views(w_grouped[unit][:], w_raw[unit][:])
            copy(out=dst, in_=src)

        def regroup_on_gpsimd(unit):
            dst, src = regrouped_views(w_grouped[unit][:], w_raw[unit][:])
            half = dst.shape[1] // 2
            for q in range(2):
                nc.gpsimd.tensor_scalar(
                    out=dst[:, q * half : (q + 1) * half, :, :],
                    in0=src[:, q * half : (q + 1) * half, :, :],
                    scalar1=1.0,
                    scalar2=0.0,
                    op0=ALU.mult,
                    op1=ALU.add,
                )

        def second_matmul(n, i):
            acc = psum.tile([P, CHUNK], F32, name="acc%d_%d" % (n, i), tag="bank")
            banks[("acc", n, i)] = acc
            for g in range(PASSES):
                nc.tensor.matmul_mx(
                    out=acc[:],
                    lhsT=act_codes[g][:, P * i : P * (i + 1)].bitcast(FP8X4),
                    lhsT_scale=act_scales[g][:, P * i : P * (i + 1)],
                    rhs=w_codes[n][:, g, :].bitcast(FP8X4),
                    rhs_scale=w_scales[n][:, g, :],
                    start=(g == 0),
                    stop=(g == PASSES - 1),
                )

        def add_bias(n, i):
            o = outs.tile([P, CHUNK], F32, name="o")
            banks[("o", n, i)] = o
            nc.vector.tensor_tensor(
                out=o[:], in0=banks[("acc", n, i)][:], in1=bias[:, n * CHUNK : (n + 1) * CHUNK], op=ALU.add
            )

        def silu_and_store(n, i):
            o = banks[("o", n, i)]
            nc.scalar.activation(out=o[:], in_=o[:], func=ACT.Silu)
            nc.sync.dma_start(out=out_rows[P * i : P * (i + 1), n * CHUNK : (n + 1) * CHUNK], in_=o[:])

        ctx.enter_context(tc.manual_schedule())

        nc.sync.dma_start(out=pre_raw[:], in_=pre1.rearrange("(j p) e -> p j e", p=P))
        load_x(0)
        load_x(1)
        load_weights(0, 0)
        load_x(2)
        load_weights(0, 1)
        load_x(3)
        nc.sync.dma_start(out=h_raw[:], in_=h.rearrange("b n d -> n b d"))
        load_weights(1, 0)
        load_weights(1, 1)
        load_weights(2, 1)
        load_weights(2, 0)
        nc.sync.dma_start(out=bias[:], in_=b1_0.partition_broadcast(P))
        for unit in GPSIMD_UNITS:
            load_weights(unit[0], unit[1])

        dst, src = regrouped_views(pre_grouped[:], pre_raw[:])
        nc.vector.tensor_copy(out=dst, in_=src)
        quantise(pre_codes[:], pre_scales[:], pre_grouped[:])
        transpose_x(0)
        copy_x(0, nc.scalar.copy)
        quantise_x(0)
        transpose_x(1)
        first_matmul(0)
        copy_x(1, nc.scalar.copy)
        quantise_x(1)
        square(0)
        first_matmul(1)
        regroup((0, 0), nc.vector.tensor_copy)
        square(1)
        transpose_x(2)
        copy_x(2, nc.vector.tensor_copy)
        quantise_x(2)
        quantise_weights((0, 0))
        norm(0)
        root_of_norm(0)
        first_matmul(2)
        transpose_x(3)
        square(2)
        regroup((0, 1), nc.vector.tensor_copy)
        quantise_inv(0)
        copy_x(3, nc.vector.tensor_copy)
        quantise_x(3)
        quantise_weights((0, 1))
        norm(1)
        root_of_norm(1)
        regroup((1, 0), nc.vector.tensor_copy)
        first_matmul(3)
        square(3)
        quantise_inv(1)
        quantise_weights((1, 0))
        regroup((1, 1), nc.vector.tensor_copy)
        norm(2)
        transpose_h()
        root_of_norm(2)
        copy_h()
        quantise_inv(2)
        quantise_weights((1, 1))
        quantise(h_codes[:], h_scales[:], h_grouped[:])
        norm(3)
        root_of_norm(3)
        regroup((2, 0), nc.vector.tensor_copy)
        quantise_inv(3)
        regroup((2, 1), nc.scalar.copy)
        for i in range(TOKEN_TILES):
            second_matmul(0, i)
        quantise_weights((2, 0))
        quantise_weights((2, 1))
        for unit in GPSIMD_UNITS:
            regroup_on_gpsimd(unit)
        for i in range(TOKEN_TILES):
            add_bias(0, i)
            silu_and_store(0, i)
        for i in range(TOKEN_TILES):
            second_matmul(1, i)
        for i in range(TOKEN_TILES):
            add_bias(1, i)
            silu_and_store(1, i)
        for n in (2, 3):
            for i in range(TOKEN_TILES):
                second_matmul(n, i)
                add_bias(n, i)
                silu_and_store(n, i)
                if n == 2 and i < 2:
                    quantise_weights(GPSIMD_UNITS[i])
